import numpy as np
import ml_dtypes


def mxq(x, axis, fmt="e4m3"):
    dtype, down = {"e4m3": (ml_dtypes.float8_e4m3fn, 7), "e5m2": (ml_dtypes.float8_e5m2, 14)}[fmt]
    v = np.moveaxis(np.asarray(x, np.float32).astype(ml_dtypes.bfloat16).astype(np.float64), axis, -1)
    blocks = v.reshape(v.shape[:-1] + (-1, 32))
    amax = np.abs(blocks).max(-1, keepdims=True)
    byte = np.maximum(np.where(amax > 0, np.frexp(amax)[1] - 1 + 127, 0) - down, 1)
    scale = np.exp2(byte - 127.0)
    codes = (blocks / scale).astype(np.float32).astype(dtype).astype(np.float64)
    return np.moveaxis((codes * scale).reshape(v.shape), -1, axis)


WIDE = False


def mx_kscale(k):
    if not WIDE:
        return np.ones(k)
    levels = np.array([10, -10, 5, -5, 0])
    a = np.random.permutation(np.resize(levels, k // 512 * 4)).reshape(k // 512, 4)
    idx = np.arange(k)
    return np.exp2(a[idx // 512, idx % 128 // 32])


BF16 = ml_dtypes.bfloat16


def bf(x):
    return np.asarray(x, np.float32).astype(BF16)


def f64(x):
    return np.asarray(x).astype(np.float64)


E2M1 = np.array([0.0, 0.5, 1.0, 1.5, 2.0, 3.0, 4.0, 6.0, -0.0, -0.5, -1.0, -1.5, -2.0, -3.0, -4.0, -6.0])


def pack_weight(w, fmt):
    k, n = w.shape
    w = f64(bf(w)).reshape(k // 32, 32, n)
    amax = np.abs(w).max(1)
    if fmt == "e4m3":
        byte = np.frexp(amax)[1] - 1 + 127 - 7
    else:
        mant, ex = np.frexp(amax / 6.0)
        byte = np.where(mant > 0.5, ex, ex - 1) + 127
    byte = np.clip(np.where(amax > 0, byte, 1), 1, 254)
    scaled = (w * np.exp2(127.0 - byte)[:, None, :]).reshape(k, n).astype(np.float32)
    by_word = np.ascontiguousarray(scaled.reshape(k // 512, 128, 4, n).transpose(0, 1, 3, 2))
    if fmt == "e4m3":
        words = by_word.astype(ml_dtypes.float8_e4m3fn).view(np.uint8)
    else:
        c = by_word.astype(ml_dtypes.float4_e2m1fn).view(np.uint8) & 0xF
        words = c[..., 0::2] | (c[..., 1::2] << 4)
    return np.ascontiguousarray(words), np.ascontiguousarray(byte.astype(np.uint8).reshape(k // 512, 16, n))


def unpack_weight(words, scales, fmt):
    g, p, n, _ = words.shape
    if fmt == "e4m3":
        vals = np.ascontiguousarray(words).view(ml_dtypes.float8_e4m3fn).astype(np.float64)
    else:
        nib = np.empty((g, p, n, 4), np.uint8)
        nib[..., 0::2] = words & 0xF
        nib[..., 1::2] = words >> 4
        vals = E2M1[nib]
    vals = vals * np.repeat(np.exp2(scales.astype(np.float64) - 127.0), 8, axis=1)[..., None]
    return vals.transpose(0, 1, 3, 2).reshape(g * 512, n)

def pack4(w):
    words, scales = pack_weight(w, "e2m1")
    return words.reshape(words.shape[0], 128, -1), scales


def unpack4(words, scales):
    return unpack_weight(words.reshape(words.shape[0], 128, -1, 2), scales, "e2m1")


B, CIN, H, W, CR, COUT, SP, K = 4, 2048, 8, 8, 512, 2048, 8, 7
PAD = K // 2
KK = K * K
HN = COUT // SP
HW = H * W
OFFS = [(dy, dx) for dy in range(K) for dx in range(K)]


def setup_inputs():
    s = mx_kscale(CIN)
    logits = bf(np.random.standard_normal((B, HN, KK, HW)) * 1.5)
    x = bf(np.random.standard_normal((B, CIN, H, W)) * s[None, :, None, None])
    w3c = np.random.standard_normal((COUT, CIN)) * 2.0 / np.sqrt(CIN) / s[None, :]
    b3c = bf(np.random.standard_normal(COUT) * 0.5)
    words, scales = pack4(np.ascontiguousarray(w3c.T))
    return {
        "logits": logits,
        "x": x,
        "w3c_words": words,
        "w3c_scales": scales,
        "b3c": b3c,
    }


def reference(logits, x, w3c_words, w3c_scales, b3c):
    x3 = (unpack4(w3c_words, w3c_scales).T @ mxq(f64(x).reshape(B, CIN, HW), 1, "e4m3")) + f64(b3c)[None, :, None]
    x3 = x3.reshape(B, COUT, H, W)
    lg = f64(logits)
    e = np.exp(lg - lg.max(axis=2, keepdims=True))
    wgt = (e / e.sum(axis=2, keepdims=True)).reshape(B, HN, KK, H, W)
    x3p = np.pad(x3, ((0, 0), (0, 0), (PAD, PAD), (PAD, PAD)), mode="reflect")
    acc = np.zeros((B, HN, SP, H, W))
    for k, (dy, dx) in enumerate(OFFS):
        patch = x3p[:, :, dy:dy + H, dx:dx + W].reshape(B, HN, SP, H, W)
        acc = acc + patch * wgt[:, :, k][:, :, None]
    return acc.reshape(B, COUT, H, W)

@@ -1,0 +1,214 @@
+from contextlib import ExitStack
+
+import concourse.mybir as mybir
+from concourse.masks import make_identity
+
+F32 = mybir.dt.float32
+BF16 = mybir.dt.bfloat16
+I32 = mybir.dt.int32
+U32 = mybir.dt.uint32
+U8 = mybir.dt.uint8
+FP8X4 = mybir.dt.float8_e4m3fn_x4
+FP4X4 = mybir.dt.float4_e2m1fn_x4
+ALU = mybir.AluOpType
+ACT = mybir.ActivationFunctionType
+AXIS = mybir.AxisListType
+
+P = 128
+PACK = 4
+K_PASS = P * PACK
+B, CIN, SIDE, COUT, SP, WIN = 4, 2048, 8, 2048, 8, 7
+HW = SIDE * SIDE
+KK = WIN * WIN
+PAD = WIN // 2
+PASSES = CIN // K_PASS
+N_TILE = 512
+HEAD_GROUPS = COUT // SP // P
+MARGIN = PAD
+
+FLOPS = 2 * B * HW * CIN * COUT + 2 * B * COUT * HW * KK
+
+
+def outside_offsets():
+    found = []
+    for pos in range(SIDE):
+        for off in range(WIN):
+            u = pos + off - PAD
+            if u < 0:
+                found.append((pos, off, -u - pos + PAD))
+            elif u > SIDE - 1:
+                found.append((pos, off, 2 * (SIDE - 1) - u - pos + PAD))
+    return found
+
+
+def tile_sam_pb_kernel(tc, logits, x, w3c_words, w3c_scales, b3c, out):
+    nc = tc.nc
+    with ExitStack() as ctx:
+        keep = ctx.enter_context(tc.tile_pool(name="keep", bufs=1))
+        stream = ctx.enter_context(tc.tile_pool(name="stream", bufs=2))
+        mx_psum = ctx.enter_context(tc.psum_pool(name="mx_psum", bufs=4))
+        tr_psum = ctx.enter_context(tc.psum_pool(name="tr_psum", bufs=2))
+
+        x_raw = keep.tile([P, B, PASSES, PACK, HW], BF16)
+        nc.sync.dma_start(
+            out=x_raw[:], in_=x.rearrange("b (g p t) i j -> p b g t (i j)", g=PASSES, p=P, t=PACK)
+        )
+        x_grouped = keep.tile([P, PASSES, B * HW, PACK], BF16, align_bytes=64)
+        x_codes = keep.tile([P, PASSES, B * HW], U32, align_bytes=64)
+        x_scales = keep.tile([P, PASSES, B * HW], U8, align_bytes=64)
+        for g in range(PASSES):
+            nc.vector.tensor_copy(
+                out=x_grouped[:, g].rearrange("p (b n) t -> p b n t", b=B),
+                in_=x_raw[:, :, g].rearrange("p b t n -> p b n t"),
+            )
+        for g in range(PASSES):
+            nc.vector.quantize_mx(
+                out=x_codes[:, g, :].bitcast(FP8X4),
+                scales=x_scales[:, g, :],
+                in_=x_grouped[:, g].rearrange("p c t -> p (c t)"),
+            )
+
+        w_scales = keep.tile([P, PASSES, COUT], U8, align_bytes=64)
+        nc.vector.memset(w_scales[:].rearrange("p g n -> p (g n)").bitcast(I32), 0)
+        for half in range(2):
+            for r in range(4):
+                nc.sync.dma_start(
+                    out=w_scales[32 * half + r : P : 64, :, :].bitcast(I32),
+                    in_=w3c_scales[:, 4 * half + r : 16 : 8, :].rearrange("g q n -> q g n").bitcast(I32),
+                )
+        w_words = keep.tile([P, PASSES, 2 * COUT], U8, align_bytes=64)
+        for g in range(PASSES):
+            nc.sync.dma_start(out=w_words[:, g, :].bitcast(I32), in_=w3c_words[g].bitcast(I32))
+
+        bias_bf = keep.tile([P, HEAD_GROUPS, SP], BF16)
+        nc.scalar.dma_start(out=bias_bf[:], in_=b3c.rearrange("(g r s) -> r g s", g=HEAD_GROUPS, r=P))
+        bias = keep.tile([P, HEAD_GROUPS, SP], F32)
+        nc.vector.tensor_copy(out=bias[:], in_=bias_bf[:])
+
+        identity = keep.tile([P, P], F32)
+        make_identity(nc, identity[:])
+
+        x3T = keep.tile([P, B // 2, SP, COUT // SP], F32)
+        heads_per_tile = N_TILE // SP
+        for pair in range(B // 2):
+            cols = slice(P * pair, P * (pair + 1))
+            for ot in range(COUT // N_TILE):
+                acc = mx_psum.tile([P, N_TILE], F32)
+                for g in range(PASSES):
+                    nc.tensor.matmul_mx(
+                        out=acc[:],
+                        lhsT=x_codes[:, g, cols].bitcast(FP8X4),
+                        lhsT_scale=x_scales[:, g, cols],
+                        rhs=w_words[:, g, 2 * N_TILE * ot : 2 * N_TILE * (ot + 1)].bitcast(FP4X4),
+                        rhs_scale=w_scales[:, g, N_TILE * ot : N_TILE * (ot + 1)],
+                        start=(g == 0),
+                        stop=(g == PASSES - 1),
+                    )
+                nc.scalar.copy(
+                    out=x3T[:, pair, :, heads_per_tile * ot : heads_per_tile * (ot + 1)],
+                    in_=acc[:].rearrange("p (h s) -> p s h", s=SP),
+                )
+
+        x3 = keep.tile([P, HEAD_GROUPS, B, SP, MARGIN + HW + MARGIN], F32)
+        nc.gpsimd.memset(x3[:], 0.0)
+        for pair in range(B // 2):
+            for hg in range(HEAD_GROUPS):
+                for s0 in range(0, SP, 4):
+                    flipped = tr_psum.tile([P, 4, P], F32)
+                    for k in range(4):
+                        nc.tensor.transpose(
+                            flipped[:, k, :], x3T[:, pair, s0 + k, P * hg : P * (hg + 1)], identity[:]
+                        )
+                    nc.scalar.copy(
+                        out=x3[:, hg, 2 * pair : 2 * pair + 2, s0 : s0 + 4, MARGIN : MARGIN + HW].rearrange(
+                            "p x s m -> p s x m"
+                        ),
+                        in_=flipped[:].rearrange("p s (x m) -> p s x m", x=2),
+                    )
+
+        folds = outside_offsets()
+        for hg in range(HEAD_GROUPS):
+            heads = slice(P * hg, P * (hg + 1))
+            for pair in range(B // 2):
+                lg = stream.tile([P, 2, KK, HW], BF16)
+                for xb in range(2):
+                    nc.sync.dma_start(out=lg[:, xb], in_=logits[2 * pair + xb, heads])
+                top = stream.tile([P, 2, KK // 2, HW], BF16)
+                nc.vector.tensor_tensor(
+                    out=top[:], in0=lg[:, :, 0 : KK // 2, :], in1=lg[:, :, KK // 2 + 1 : KK, :], op=ALU.max
+                )
+                rows = KK // 2
+                while rows > 1:
+                    half = rows // 2
+                    nc.vector.tensor_tensor(
+                        out=top[:, :, 0:half, :],
+                        in0=top[:, :, 0:half, :],
+                        in1=top[:, :, rows - half : rows, :],
+                        op=ALU.max,
+                    )
+                    rows = rows - half
+                nc.vector.tensor_tensor(
+                    out=top[:, :, 0:1, :], in0=top[:, :, 0:1, :], in1=lg[:, :, KK // 2 : KK // 2 + 1, :], op=ALU.max
+                )
+                e = stream.tile([P, 2, KK, HW], F32)
+                nc.vector.tensor_tensor(
+                    out=e[:], in0=lg[:], in1=top[:, :, 0:1, :].to_broadcast([P, 2, KK, HW]), op=ALU.subtract
+                )
+                nc.scalar.activation(out=e[:], in_=e[:], func=ACT.Exp)
+                total = stream.tile([P, 2, HW], F32)
+                nc.vector.tensor_reduce(
+                    out=total[:], in_=e[:].rearrange("p x l n -> p x n l"), axis=AXIS.X, op=ALU.add
+                )
+                inv_total = stream.tile([P, 2, HW], F32)
+                nc.vector.reciprocal(out=inv_total[:], in_=total[:])
+
+                e6 = e[:].rearrange("p x (dy dx) (i j) -> p x dy dx i j", dy=WIN, i=SIDE)
+                for i, src, dst in folds:
+                    nc.vector.tensor_tensor(
+                        out=e6[:, :, dst, :, i, :], in0=e6[:, :, dst, :, i, :], in1=e6[:, :, src, :, i, :], op=ALU.add
+                    )
+                for j, src, dst in folds:
+                    nc.vector.tensor_tensor(
+                        out=e6[:, :, :, dst, :, j], in0=e6[:, :, :, dst, :, j], in1=e6[:, :, :, src, :, j], op=ALU.add
+                    )
+                for j, src, dst in folds:
+                    nc.vector.memset(e6[:, :, :, src, :, j], 0.0)
+
+                for xb in range(2):
+                    b = 2 * pair + xb
+                    sums = stream.tile([P, WIN, SP, HW], F32)
+                    for dy in [PAD] + [d for d in range(WIN) if d != PAD]:
+                        first_row = max(0, PAD - dy)
+                        last_row = min(SIDE - 1, SIDE - 1 + PAD - dy)
+                        n0 = SIDE * first_row
+                        n1 = SIDE * (last_row + 1)
+                        if dy == PAD:
+                            prod = sums
+                        else:
+                            prod = stream.tile([P, WIN, SP, HW], F32, name="prod")
+                        for dx in range(WIN):
+                            shift = MARGIN + SIDE * (dy - PAD) + (dx - PAD)
+                            nc.vector.tensor_tensor(
+                                out=prod[:, dx, :, n0:n1],
+                                in0=x3[:, hg, b, :, shift + n0 : shift + n1],
+                                in1=e[:, xb, WIN * dy + dx, n0:n1].unsqueeze(1).to_broadcast([P, SP, n1 - n0]),
+                                op=ALU.mult,
+                            )
+                        if dy != PAD:
+                            nc.vector.tensor_tensor(
+                                out=sums[:, :, :, n0:n1], in0=sums[:, :, :, n0:n1], in1=prod[:, :, :, n0:n1], op=ALU.add
+                            )
+                    y = stream.tile([P, SP, HW], F32)
+                    nc.vector.tensor_reduce(
+                        out=y[:], in_=sums[:].rearrange("p d s n -> p s n d"), axis=AXIS.X, op=ALU.add
+                    )
+                    nc.vector.tensor_tensor(
+                        out=y[:], in0=y[:], in1=inv_total[:, xb, :].unsqueeze(1).to_broadcast([P, SP, HW]), op=ALU.mult
+                    )
+                    nc.vector.tensor_tensor(
+                        out=y[:], in0=y[:], in1=bias[:, hg, :].unsqueeze(2).to_broadcast([P, SP, HW]), op=ALU.add
+                    )
+                    nc.sync.dma_start(
+                        out=out[b, SP * P * hg : SP * P * (hg + 1)].rearrange("(r s) i j -> r (s i j)", s=SP),
+                        in_=y[:].rearrange("p s n -> p (s n)"),
+                    )

@@ -12,7 +12,6 @@ FP8X4 = mybir.dt.float8_e4m3fn_x4
 FP4X4 = mybir.dt.float4_e2m1fn_x4
 ALU = mybir.AluOpType
 ACT = mybir.ActivationFunctionType
-AXIS = mybir.AxisListType
 
 P = 128
 PACK = 4
@@ -23,8 +22,16 @@ KK = WIN * WIN
 PAD = WIN // 2
 PASSES = CIN // K_PASS
 N_TILE = 512
-HEAD_GROUPS = COUT // SP // P
-MARGIN = PAD
+HEADS = COUT // SP
+HEAD_GROUPS = HEADS // P
+PAIRS = B // 2
+SLOTS = SIDE * SIDE
+CENTRE = SIDE * PAD + PAD
+PITCH = 2 * SLOTS + 1
+LEAD = 32 - CENTRE
+X3_COLS = 12
+Y_COLS = 16
+Y_HEADS = N_TILE // Y_COLS
 
 FLOPS = 2 * B * HW * CIN * COUT + 2 * B * COUT * HW * KK
 
@@ -43,172 +50,195 @@ def outside_offsets():
 
 def tile_sam_pb_kernel(tc, logits, x, w3c_words, w3c_scales, b3c, out):
     nc = tc.nc
+    folds = outside_offsets()
     with ExitStack() as ctx:
         keep = ctx.enter_context(tc.tile_pool(name="keep", bufs=1))
         stream = ctx.enter_context(tc.tile_pool(name="stream", bufs=2))
-        mx_psum = ctx.enter_context(tc.psum_pool(name="mx_psum", bufs=4))
-        tr_psum = ctx.enter_context(tc.psum_pool(name="tr_psum", bufs=2))
-
-        x_raw = keep.tile([P, B, PASSES, PACK, HW], BF16)
-        nc.sync.dma_start(
-            out=x_raw[:], in_=x.rearrange("b (g p t) i j -> p b g t (i j)", g=PASSES, p=P, t=PACK)
-        )
-        x_grouped = keep.tile([P, PASSES, B * HW, PACK], BF16, align_bytes=64)
-        x_codes = keep.tile([P, PASSES, B * HW], U32, align_bytes=64)
-        x_scales = keep.tile([P, PASSES, B * HW], U8, align_bytes=64)
-        for g in range(PASSES):
-            nc.vector.tensor_copy(
-                out=x_grouped[:, g].rearrange("p (b n) t -> p b n t", b=B),
-                in_=x_raw[:, :, g].rearrange("p b t n -> p b n t"),
-            )
-        for g in range(PASSES):
-            nc.vector.quantize_mx(
-                out=x_codes[:, g, :].bitcast(FP8X4),
-                scales=x_scales[:, g, :],
-                in_=x_grouped[:, g].rearrange("p c t -> p (c t)"),
-            )
-
-        w_scales = keep.tile([P, PASSES, COUT], U8, align_bytes=64)
-        nc.vector.memset(w_scales[:].rearrange("p g n -> p (g n)").bitcast(I32), 0)
-        for half in range(2):
-            for r in range(4):
-                nc.sync.dma_start(
-                    out=w_scales[32 * half + r : P : 64, :, :].bitcast(I32),
-                    in_=w3c_scales[:, 4 * half + r : 16 : 8, :].rearrange("g q n -> q g n").bitcast(I32),
-                )
-        w_words = keep.tile([P, PASSES, 2 * COUT], U8, align_bytes=64)
-        for g in range(PASSES):
-            nc.sync.dma_start(out=w_words[:, g, :].bitcast(I32), in_=w3c_words[g].bitcast(I32))
-
-        bias_bf = keep.tile([P, HEAD_GROUPS, SP], BF16)
-        nc.scalar.dma_start(out=bias_bf[:], in_=b3c.rearrange("(g r s) -> r g s", g=HEAD_GROUPS, r=P))
-        bias = keep.tile([P, HEAD_GROUPS, SP], F32)
-        nc.vector.tensor_copy(out=bias[:], in_=bias_bf[:])
+        mx_psum = ctx.enter_context(tc.psum_pool(name="mx_psum", bufs=2))
+        tr_psum = ctx.enter_context(tc.psum_pool(name="tr_psum", bufs=3))
+        y_psum = ctx.enter_context(tc.psum_pool(name="y_psum", bufs=2))
+        back_psum = ctx.enter_context(tc.psum_pool(name="back_psum", bufs=1))
 
         identity = keep.tile([P, P], F32)
         make_identity(nc, identity[:])
 
-        x3T = keep.tile([P, B // 2, SP, COUT // SP], F32)
-        heads_per_tile = N_TILE // SP
-        for pair in range(B // 2):
-            cols = slice(P * pair, P * (pair + 1))
-            for ot in range(COUT // N_TILE):
-                acc = mx_psum.tile([P, N_TILE], F32)
-                for g in range(PASSES):
-                    nc.tensor.matmul_mx(
-                        out=acc[:],
-                        lhsT=x_codes[:, g, cols].bitcast(FP8X4),
-                        lhsT_scale=x_scales[:, g, cols],
-                        rhs=w_words[:, g, 2 * N_TILE * ot : 2 * N_TILE * (ot + 1)].bitcast(FP4X4),
-                        rhs_scale=w_scales[:, g, N_TILE * ot : N_TILE * (ot + 1)],
-                        start=(g == 0),
-                        stop=(g == PASSES - 1),
-                    )
-                nc.scalar.copy(
-                    out=x3T[:, pair, :, heads_per_tile * ot : heads_per_tile * (ot + 1)],
-                    in_=acc[:].rearrange("p (h s) -> p s h", s=SP),
-                )
+        skewed = keep.tile([P, LEAD + HW * PITCH], F32)
+        nc.vector.memset(skewed[:], 0.0)
+        by_position = skewed[:, LEAD:].rearrange("p (n c) -> p n c", c=PITCH)
+        slots6 = by_position[:, :, 0 : 2 * SLOTS].rearrange(
+            "p (i j) (x dy dx) -> p i j x dy dx", i=SIDE, x=2, dy=SIDE
+        )
 
-        x3 = keep.tile([P, HEAD_GROUPS, B, SP, MARGIN + HW + MARGIN], F32)
-        nc.gpsimd.memset(x3[:], 0.0)
-        for pair in range(B // 2):
-            for hg in range(HEAD_GROUPS):
-                for s0 in range(0, SP, 4):
-                    flipped = tr_psum.tile([P, 4, P], F32)
-                    for k in range(4):
-                        nc.tensor.transpose(
-                            flipped[:, k, :], x3T[:, pair, s0 + k, P * hg : P * (hg + 1)], identity[:]
-                        )
-                    nc.scalar.copy(
-                        out=x3[:, hg, 2 * pair : 2 * pair + 2, s0 : s0 + 4, MARGIN : MARGIN + HW].rearrange(
-                            "p x s m -> p s x m"
-                        ),
-                        in_=flipped[:].rearrange("p s (x m) -> p s x m", x=2),
-                    )
-
-        folds = outside_offsets()
-        for hg in range(HEAD_GROUPS):
-            heads = slice(P * hg, P * (hg + 1))
-            for pair in range(B // 2):
-                lg = stream.tile([P, 2, KK, HW], BF16)
-                for xb in range(2):
-                    nc.sync.dma_start(out=lg[:, xb], in_=logits[2 * pair + xb, heads])
-                top = stream.tile([P, 2, KK // 2, HW], BF16)
+        def softmax_numerators(hg, pair):
+            for xb in range(2):
+                lg = stream.tile([P, KK, HW], BF16, name="lg")
+                nc.sync.dma_start(out=lg[:], in_=logits[2 * pair + xb, P * hg : P * (hg + 1)])
+                top = stream.tile([P, KK // 2, HW], BF16, name="top")
                 nc.vector.tensor_tensor(
-                    out=top[:], in0=lg[:, :, 0 : KK // 2, :], in1=lg[:, :, KK // 2 + 1 : KK, :], op=ALU.max
+                    out=top[:], in0=lg[:, 0 : KK // 2, :], in1=lg[:, KK // 2 + 1 : KK, :], op=ALU.max
                 )
                 rows = KK // 2
                 while rows > 1:
                     half = rows // 2
                     nc.vector.tensor_tensor(
-                        out=top[:, :, 0:half, :],
-                        in0=top[:, :, 0:half, :],
-                        in1=top[:, :, rows - half : rows, :],
-                        op=ALU.max,
+                        out=top[:, 0:half, :], in0=top[:, 0:half, :], in1=top[:, rows - half : rows, :], op=ALU.max
                     )
                     rows = rows - half
                 nc.vector.tensor_tensor(
-                    out=top[:, :, 0:1, :], in0=top[:, :, 0:1, :], in1=lg[:, :, KK // 2 : KK // 2 + 1, :], op=ALU.max
+                    out=top[:, 0:1, :], in0=top[:, 0:1, :], in1=lg[:, KK // 2 : KK // 2 + 1, :], op=ALU.max
                 )
-                e = stream.tile([P, 2, KK, HW], F32)
+                diff = stream.tile([P, KK, HW], F32, name="diff")
                 nc.vector.tensor_tensor(
-                    out=e[:], in0=lg[:], in1=top[:, :, 0:1, :].to_broadcast([P, 2, KK, HW]), op=ALU.subtract
+                    out=diff[:], in0=lg[:], in1=top[:, 0:1, :].to_broadcast([P, KK, HW]), op=ALU.subtract
                 )
-                nc.scalar.activation(out=e[:], in_=e[:], func=ACT.Exp)
-                total = stream.tile([P, 2, HW], F32)
-                nc.vector.tensor_reduce(
-                    out=total[:], in_=e[:].rearrange("p x l n -> p x n l"), axis=AXIS.X, op=ALU.add
+                nc.scalar.activation(
+                    out=by_position[:, :, SLOTS * xb : SLOTS * (xb + 1)].rearrange("p n (dy dx) -> p n dy dx", dy=SIDE)[
+                        :, :, 0:WIN, 0:WIN
+                    ],
+                    in_=diff[:].rearrange("p (dy dx) n -> p n dy dx", dy=WIN),
+                    func=ACT.Exp,
                 )
-                inv_total = stream.tile([P, 2, HW], F32)
-                nc.vector.reciprocal(out=inv_total[:], in_=total[:])
+            for i, src, dst in folds:
+                nc.gpsimd.tensor_tensor(
+                    out=slots6[:, i, :, :, dst, 0:WIN],
+                    in0=slots6[:, i, :, :, dst, 0:WIN],
+                    in1=slots6[:, i, :, :, src, 0:WIN],
+                    op=ALU.add,
+                )
+            for i, src, dst in folds:
+                nc.gpsimd.memset(slots6[:, i, :, :, src, 0:WIN], 0.0)
+            for j, src, dst in folds:
+                nc.gpsimd.tensor_tensor(
+                    out=slots6[:, :, j, :, 0:WIN, dst],
+                    in0=slots6[:, :, j, :, 0:WIN, dst],
+                    in1=slots6[:, :, j, :, 0:WIN, src],
+                    op=ALU.add,
+                )
+            for j, src, dst in folds:
+                nc.gpsimd.memset(slots6[:, :, j, :, 0:WIN, src], 0.0)
 
-                e6 = e[:].rearrange("p x (dy dx) (i j) -> p x dy dx i j", dy=WIN, i=SIDE)
-                for i, src, dst in folds:
-                    nc.vector.tensor_tensor(
-                        out=e6[:, :, dst, :, i, :], in0=e6[:, :, dst, :, i, :], in1=e6[:, :, src, :, i, :], op=ALU.add
-                    )
-                for j, src, dst in folds:
-                    nc.vector.tensor_tensor(
-                        out=e6[:, :, :, dst, :, j], in0=e6[:, :, :, dst, :, j], in1=e6[:, :, :, src, :, j], op=ALU.add
-                    )
-                for j, src, dst in folds:
-                    nc.vector.memset(e6[:, :, :, src, :, j], 0.0)
+        softmax_numerators(0, 0)
 
-                for xb in range(2):
-                    b = 2 * pair + xb
-                    sums = stream.tile([P, WIN, SP, HW], F32)
-                    for dy in [PAD] + [d for d in range(WIN) if d != PAD]:
-                        first_row = max(0, PAD - dy)
-                        last_row = min(SIDE - 1, SIDE - 1 + PAD - dy)
-                        n0 = SIDE * first_row
-                        n1 = SIDE * (last_row + 1)
-                        if dy == PAD:
-                            prod = sums
-                        else:
-                            prod = stream.tile([P, WIN, SP, HW], F32, name="prod")
-                        for dx in range(WIN):
-                            shift = MARGIN + SIDE * (dy - PAD) + (dx - PAD)
-                            nc.vector.tensor_tensor(
-                                out=prod[:, dx, :, n0:n1],
-                                in0=x3[:, hg, b, :, shift + n0 : shift + n1],
-                                in1=e[:, xb, WIN * dy + dx, n0:n1].unsqueeze(1).to_broadcast([P, SP, n1 - n0]),
-                                op=ALU.mult,
-                            )
-                        if dy != PAD:
-                            nc.vector.tensor_tensor(
-                                out=sums[:, :, :, n0:n1], in0=sums[:, :, :, n0:n1], in1=prod[:, :, :, n0:n1], op=ALU.add
-                            )
-                    y = stream.tile([P, SP, HW], F32)
-                    nc.vector.tensor_reduce(
-                        out=y[:], in_=sums[:].rearrange("p d s n -> p s n d"), axis=AXIS.X, op=ALU.add
-                    )
-                    nc.vector.tensor_tensor(
-                        out=y[:], in0=y[:], in1=inv_total[:, xb, :].unsqueeze(1).to_broadcast([P, SP, HW]), op=ALU.mult
-                    )
-                    nc.vector.tensor_tensor(
-                        out=y[:], in0=y[:], in1=bias[:, hg, :].unsqueeze(2).to_broadcast([P, SP, HW]), op=ALU.add
-                    )
+        x3T = keep.tile([P, PAIRS, HEADS, X3_COLS], F32)
+        nc.gpsimd.memset(x3T[:], 1.0)
+        bias_col = keep.tile([P, COUT // P], F32)
+
+        with tc.tile_pool(name="front", bufs=1) as front:
+            x_raw = front.tile([P, B, PASSES, PACK, HW], BF16)
+            nc.sync.dma_start(
+                out=x_raw[:], in_=x.rearrange("b (g p t) i j -> p b g t (i j)", g=PASSES, p=P, t=PACK)
+            )
+            x_grouped = front.tile([P, PASSES, B * HW, PACK], BF16, align_bytes=64)
+            x_codes = front.tile([P, PASSES, B * HW], U32, align_bytes=64)
+            x_scales = front.tile([P, PASSES, B * HW], U8, align_bytes=64)
+            for g in range(PASSES):
+                nc.vector.tensor_copy(
+                    out=x_grouped[:, g].rearrange("p (b n) t -> p b n t", b=B),
+                    in_=x_raw[:, :, g].rearrange("p b t n -> p b n t"),
+                )
+            for g in range(PASSES):
+                nc.vector.quantize_mx(
+                    out=x_codes[:, g, :].bitcast(FP8X4),
+                    scales=x_scales[:, g, :],
+                    in_=x_grouped[:, g].rearrange("p c t -> p (c t)"),
+                )
+
+            w_scales = front.tile([P, PASSES, COUT], U8, align_bytes=64)
+            nc.vector.memset(w_scales[:].rearrange("p g n -> p (g n)").bitcast(I32), 0)
+            for half in range(2):
+                for r in range(4):
                     nc.sync.dma_start(
-                        out=out[b, SP * P * hg : SP * P * (hg + 1)].rearrange("(r s) i j -> r (s i j)", s=SP),
-                        in_=y[:].rearrange("p s n -> p (s n)"),
+                        out=w_scales[32 * half + r : P : 64, :, :].bitcast(I32),
+                        in_=w3c_scales[:, 4 * half + r : 16 : 8, :].rearrange("g q n -> q g n").bitcast(I32),
                     )
+            w_words = front.tile([P, PASSES, 2 * COUT], U8, align_bytes=64)
+            for g in range(PASSES):
+                nc.sync.dma_start(out=w_words[:, g, :].bitcast(I32), in_=w3c_words[g].bitcast(I32))
+
+            bias_bf = front.tile([COUT // P, P], BF16)
+            nc.sync.dma_start(out=bias_bf[:], in_=b3c.rearrange("(t o) -> t o", o=P))
+            bias_rows = front.tile([P, P], F32)
+            nc.vector.memset(bias_rows[:], 0.0)
+            nc.vector.tensor_copy(out=bias_rows[0 : COUT // P, :], in_=bias_bf[:])
+            bias_ps = back_psum.tile([P, 4, P], F32, name="back")
+            nc.tensor.transpose(bias_ps[:, 0, :], bias_rows[:], identity[:])
+            nc.vector.tensor_copy(out=bias_col[:], in_=bias_ps[:, 0, 0 : COUT // P])
+
+            heads_per_tile = N_TILE // SP
+            for pair in range(PAIRS):
+                cols = slice(P * pair, P * (pair + 1))
+                for ot in range(COUT // N_TILE):
+                    acc = mx_psum.tile([P, N_TILE], F32)
+                    for g in range(PASSES):
+                        nc.tensor.matmul_mx(
+                            out=acc[:],
+                            lhsT=x_codes[:, g, cols].bitcast(FP8X4),
+                            lhsT_scale=x_scales[:, g, cols],
+                            rhs=w_words[:, g, 2 * N_TILE * ot : 2 * N_TILE * (ot + 1)].bitcast(FP4X4),
+                            rhs_scale=w_scales[:, g, N_TILE * ot : N_TILE * (ot + 1)],
+                            start=(g == 0),
+                            stop=(g == PASSES - 1),
+                        )
+                    nc.scalar.copy(
+                        out=x3T[:, pair, heads_per_tile * ot : heads_per_tile * (ot + 1), 0:SP],
+                        in_=acc[:].rearrange("p (h s) -> p h s", s=SP),
+                    )
+
+        blocks_pool = ctx.enter_context(tc.tile_pool(name="blocks", bufs=1))
+        blocks = blocks_pool.tile([P, P, P], F32)
+        nc.gpsimd.memset(blocks[0:HW, :, HW:P], 0.0)
+        nc.gpsimd.memset(blocks[HW:P, :, 0:HW], 0.0)
+
+        units = [(hg, pair) for hg in range(HEAD_GROUPS) for pair in range(PAIRS)]
+        for u, (hg, pair) in enumerate(units):
+            for n0 in range(0, HW, 4):
+                flipped = tr_psum.tile([P, 4, P], F32)
+                for k in range(4):
+                    first = LEAD + CENTRE + P * (n0 + k)
+                    nc.tensor.transpose(flipped[:, k, :], skewed[:, first : first + P], identity[:])
+                nc.vector.tensor_copy(
+                    out=blocks[0:HW, :, n0 : n0 + 4], in_=flipped[0:HW].rearrange("p k r -> p r k")
+                )
+                nc.scalar.copy(
+                    out=blocks[HW:P, :, HW + n0 : HW + n0 + 4], in_=flipped[HW:P].rearrange("p k r -> p r k")
+                )
+            if u + 1 < len(units):
+                softmax_numerators(units[u + 1][0], units[u + 1][1])
+
+            y = stream.tile([P, P, SP], F32, name="y")
+            for r0 in range(0, P, Y_HEADS):
+                sums = y_psum.tile([P, Y_HEADS, Y_COLS], F32)
+                for k in range(Y_HEADS):
+                    nc.tensor.matmul(
+                        out=sums[:, k, 0 : SP + 1],
+                        lhsT=blocks[:, r0 + k, :],
+                        rhs=x3T[:, pair, P * hg + r0 + k, 0 : SP + 1],
+                        start=True,
+                        stop=True,
+                    )
+                inv_total = stream.tile([P, Y_HEADS, 1], F32, name="inv_total")
+                nc.vector.reciprocal(out=inv_total[:], in_=sums[:, :, SP : SP + 1])
+                nc.vector.tensor_tensor(
+                    out=y[:, r0 : r0 + Y_HEADS, :],
+                    in0=sums[:, :, 0:SP],
+                    in1=inv_total[:].to_broadcast([P, Y_HEADS, SP]),
+                    op=ALU.mult,
+                )
+
+            result = stream.tile([P, SP, 2, HW], F32, name="result")
+            y_cols = y[:].rearrange("p r s -> p (r s)")
+            for t0 in range(0, SP, 4):
+                back = back_psum.tile([P, 4, P], F32, name="back")
+                for k in range(4):
+                    nc.tensor.transpose(back[:, k, :], y_cols[:, P * (t0 + k) : P * (t0 + k + 1)], identity[:])
+                nc.vector.tensor_tensor(
+                    out=result[:, t0 : t0 + 4].rearrange("p t x n -> p t (x n)"),
+                    in0=back[:],
+                    in1=bias_col[:, SP * hg + t0 : SP * hg + t0 + 4].unsqueeze(2).to_broadcast([P, 4, P]),
+                    op=ALU.add,
+                )
+            for xb in range(2):
+                nc.sync.dma_start(
+                    out=out[2 * pair + xb, SP * P * hg : SP * P * (hg + 1)].rearrange("(t o) i j -> o t (i j)", o=P),
+                    in_=result[:, :, xb, :],
+                )

@@ -22,16 +22,9 @@ KK = WIN * WIN
 PAD = WIN // 2
 PASSES = CIN // K_PASS
 N_TILE = 512
-HEADS = COUT // SP
-HEAD_GROUPS = HEADS // P
-PAIRS = B // 2
-SLOTS = SIDE * SIDE
-CENTRE = SIDE * PAD + PAD
-PITCH = 2 * SLOTS + 1
-LEAD = 32 - CENTRE
-X3_COLS = 12
-Y_COLS = 16
-Y_HEADS = N_TILE // Y_COLS
+HEAD_GROUPS = COUT // SP // P
+CHUNK_S = P // HW
+CHUNKS = SP // CHUNK_S
 
 FLOPS = 2 * B * HW * CIN * COUT + 2 * B * COUT * HW * KK
 
@@ -55,74 +48,78 @@ def tile_sam_pb_kernel(tc, logits, x, w3c_words, w3c_scales, b3c, out):
         keep = ctx.enter_context(tc.tile_pool(name="keep", bufs=1))
         stream = ctx.enter_context(tc.tile_pool(name="stream", bufs=2))
         mx_psum = ctx.enter_context(tc.psum_pool(name="mx_psum", bufs=2))
-        tr_psum = ctx.enter_context(tc.psum_pool(name="tr_psum", bufs=3))
-        y_psum = ctx.enter_context(tc.psum_pool(name="y_psum", bufs=2))
-        back_psum = ctx.enter_context(tc.psum_pool(name="back_psum", bufs=1))
+        x3_psum = ctx.enter_context(tc.psum_pool(name="x3_psum", bufs=2))
+        sum_psum = ctx.enter_context(tc.psum_pool(name="sum_psum", bufs=2))
+        back_psum = ctx.enter_context(tc.psum_pool(name="back_psum", bufs=2))
 
         identity = keep.tile([P, P], F32)
         make_identity(nc, identity[:])
 
-        skewed = keep.tile([P, LEAD + HW * PITCH], F32)
-        nc.vector.memset(skewed[:], 0.0)
-        by_position = skewed[:, LEAD:].rearrange("p (n c) -> p n c", c=PITCH)
-        slots6 = by_position[:, :, 0 : 2 * SLOTS].rearrange(
-            "p (i j) (x dy dx) -> p i j x dy dx", i=SIDE, x=2, dy=SIDE
-        )
-
         def softmax_numerators(hg, pair):
+            lg = stream.tile([P, 2, KK, HW], BF16, name="lg")
             for xb in range(2):
-                lg = stream.tile([P, KK, HW], BF16, name="lg")
-                nc.sync.dma_start(out=lg[:], in_=logits[2 * pair + xb, P * hg : P * (hg + 1)])
-                top = stream.tile([P, KK // 2, HW], BF16, name="top")
+                nc.sync.dma_start(out=lg[:, xb], in_=logits[2 * pair + xb, P * hg : P * (hg + 1)])
+            top = keep.tile([P, 2, KK // 2, HW], BF16, name="top")
+            nc.vector.tensor_tensor(
+                out=top[:], in0=lg[:, :, 0 : KK // 2, :], in1=lg[:, :, KK // 2 + 1 : KK, :], op=ALU.max
+            )
+            rows = KK // 2
+            while rows > 1:
+                half = rows // 2
                 nc.vector.tensor_tensor(
-                    out=top[:], in0=lg[:, 0 : KK // 2, :], in1=lg[:, KK // 2 + 1 : KK, :], op=ALU.max
+                    out=top[:, :, 0:half, :],
+                    in0=top[:, :, 0:half, :],
+                    in1=top[:, :, rows - half : rows, :],
+                    op=ALU.max,
                 )
-                rows = KK // 2
-                while rows > 1:
-                    half = rows // 2
-                    nc.vector.tensor_tensor(
-                        out=top[:, 0:half, :], in0=top[:, 0:half, :], in1=top[:, rows - half : rows, :], op=ALU.max
-                    )
-                    rows = rows - half
-                nc.vector.tensor_tensor(
-                    out=top[:, 0:1, :], in0=top[:, 0:1, :], in1=lg[:, KK // 2 : KK // 2 + 1, :], op=ALU.max
-                )
-                diff = stream.tile([P, KK, HW], F32, name="diff")
-                nc.vector.tensor_tensor(
-                    out=diff[:], in0=lg[:], in1=top[:, 0:1, :].to_broadcast([P, KK, HW]), op=ALU.subtract
-                )
-                nc.scalar.activation(
-                    out=by_position[:, :, SLOTS * xb : SLOTS * (xb + 1)].rearrange("p n (dy dx) -> p n dy dx", dy=SIDE)[
-                        :, :, 0:WIN, 0:WIN
-                    ],
-                    in_=diff[:].rearrange("p (dy dx) n -> p n dy dx", dy=WIN),
-                    func=ACT.Exp,
-                )
-            for i, src, dst in folds:
+                rows = rows - half
+            nc.vector.tensor_tensor(
+                out=top[:, :, 0:1, :], in0=top[:, :, 0:1, :], in1=lg[:, :, KK // 2 : KK // 2 + 1, :], op=ALU.max
+            )
+            e = stream.tile([P, 2, KK, HW], F32, name="e")
+            nc.gpsimd.tensor_tensor(
+                out=e[:], in0=lg[:], in1=top[:, :, 0:1, :].to_broadcast([P, 2, KK, HW]), op=ALU.subtract
+            )
+            nc.scalar.activation(out=e[:], in_=e[:], func=ACT.Exp)
+            part = keep.tile([P, 2, KK // 2, HW], F32, name="part")
+            nc.gpsimd.tensor_tensor(
+                out=part[:], in0=e[:, :, 0 : KK // 2, :], in1=e[:, :, KK // 2 + 1 : KK, :], op=ALU.add
+            )
+            rows = KK // 2
+            while rows > 1:
+                half = rows // 2
                 nc.gpsimd.tensor_tensor(
-                    out=slots6[:, i, :, :, dst, 0:WIN],
-                    in0=slots6[:, i, :, :, dst, 0:WIN],
-                    in1=slots6[:, i, :, :, src, 0:WIN],
+                    out=part[:, :, 0:half, :],
+                    in0=part[:, :, 0:half, :],
+                    in1=part[:, :, rows - half : rows, :],
                     op=ALU.add,
                 )
+                rows = rows - half
+            nc.gpsimd.tensor_tensor(
+                out=part[:, :, 0:1, :], in0=part[:, :, 0:1, :], in1=e[:, :, KK // 2 : KK // 2 + 1, :], op=ALU.add
+            )
+            inv_total = stream.tile([P, 2, HW], F32, name="inv_total")
+            nc.vector.reciprocal(out=inv_total[:], in_=part[:, :, 0, :])
+            e6 = e[:].rearrange("p x (dy dx) (i j) -> p x dy dx i j", dy=WIN, i=SIDE)
             for i, src, dst in folds:
-                nc.gpsimd.memset(slots6[:, i, :, :, src, 0:WIN], 0.0)
-            for j, src, dst in folds:
                 nc.gpsimd.tensor_tensor(
-                    out=slots6[:, :, j, :, 0:WIN, dst],
-                    in0=slots6[:, :, j, :, 0:WIN, dst],
-                    in1=slots6[:, :, j, :, 0:WIN, src],
-                    op=ALU.add,
+                    out=e6[:, :, dst, :, i, :], in0=e6[:, :, dst, :, i, :], in1=e6[:, :, src, :, i, :], op=ALU.add
                 )
             for j, src, dst in folds:
-                nc.gpsimd.memset(slots6[:, :, j, :, 0:WIN, src], 0.0)
+                nc.gpsimd.tensor_tensor(
+                    out=e6[:, :, :, dst, :, j], in0=e6[:, :, :, dst, :, j], in1=e6[:, :, :, src, :, j], op=ALU.add
+                )
+            return e6, inv_total
 
-        softmax_numerators(0, 0)
+        units = [(hg, pair) for hg in range(HEAD_GROUPS) for pair in range(B // 2)]
+        ready = softmax_numerators(units[0][0], units[0][1])
 
-        x3T = keep.tile([P, PAIRS, HEADS, X3_COLS], F32)
-        nc.gpsimd.memset(x3T[:], 1.0)
-        bias_col = keep.tile([P, COUT // P], F32)
+        bias_bf = keep.tile([P, HEAD_GROUPS, SP], BF16)
+        nc.scalar.dma_start(out=bias_bf[:], in_=b3c.rearrange("(g r s) -> r g s", g=HEAD_GROUPS, r=P))
+        bias = keep.tile([P, HEAD_GROUPS, SP], F32)
+        nc.vector.tensor_copy(out=bias[:], in_=bias_bf[:])
 
+        x3T = keep.tile([P, B // 2, SP, COUT // SP], F32)
         with tc.tile_pool(name="front", bufs=1) as front:
             x_raw = front.tile([P, B, PASSES, PACK, HW], BF16)
             nc.sync.dma_start(
@@ -155,17 +152,8 @@ def tile_sam_pb_kernel(tc, logits, x, w3c_words, w3c_scales, b3c, out):
             for g in range(PASSES):
                 nc.sync.dma_start(out=w_words[:, g, :].bitcast(I32), in_=w3c_words[g].bitcast(I32))
 
-            bias_bf = front.tile([COUT // P, P], BF16)
-            nc.sync.dma_start(out=bias_bf[:], in_=b3c.rearrange("(t o) -> t o", o=P))
-            bias_rows = front.tile([P, P], F32)
-            nc.vector.memset(bias_rows[:], 0.0)
-            nc.vector.tensor_copy(out=bias_rows[0 : COUT // P, :], in_=bias_bf[:])
-            bias_ps = back_psum.tile([P, 4, P], F32, name="back")
-            nc.tensor.transpose(bias_ps[:, 0, :], bias_rows[:], identity[:])
-            nc.vector.tensor_copy(out=bias_col[:], in_=bias_ps[:, 0, 0 : COUT // P])
-
             heads_per_tile = N_TILE // SP
-            for pair in range(PAIRS):
+            for pair in range(B // 2):
                 cols = slice(P * pair, P * (pair + 1))
                 for ot in range(COUT // N_TILE):
                     acc = mx_psum.tile([P, N_TILE], F32)
@@ -180,65 +168,72 @@ def tile_sam_pb_kernel(tc, logits, x, w3c_words, w3c_scales, b3c, out):
                             stop=(g == PASSES - 1),
                         )
                     nc.scalar.copy(
-                        out=x3T[:, pair, heads_per_tile * ot : heads_per_tile * (ot + 1), 0:SP],
-                        in_=acc[:].rearrange("p (h s) -> p h s", s=SP),
+                        out=x3T[:, pair, :, heads_per_tile * ot : heads_per_tile * (ot + 1)],
+                        in_=acc[:].rearrange("p (h s) -> p s h", s=SP),
                     )
 
-        blocks_pool = ctx.enter_context(tc.tile_pool(name="blocks", bufs=1))
-        blocks = blocks_pool.tile([P, P, P], F32)
-        nc.gpsimd.memset(blocks[0:HW, :, HW:P], 0.0)
-        nc.gpsimd.memset(blocks[HW:P, :, 0:HW], 0.0)
+        products_pool = ctx.enter_context(tc.tile_pool(name="products", bufs=1))
+        products = products_pool.tile([P, KK, SP, SIDE, SIDE], F32)
+        nc.vector.memset(products[:], 0.0)
 
-        units = [(hg, pair) for hg in range(HEAD_GROUPS) for pair in range(PAIRS)]
+        x3_all = keep.tile([P, HEAD_GROUPS, B, SP, SIDE, SIDE], F32)
+        for pair in range(B // 2):
+            for hg in range(HEAD_GROUPS):
+                for s0 in range(0, SP, 4):
+                    flipped = x3_psum.tile([P, 4, P], F32)
+                    for k in range(4):
+                        nc.tensor.transpose(
+                            flipped[:, k, :], x3T[:, pair, s0 + k, P * hg : P * (hg + 1)], identity[:]
+                        )
+                    nc.scalar.copy(
+                        out=x3_all[:, hg, 2 * pair : 2 * pair + 2, s0 : s0 + 4].rearrange("p x s i j -> p s x (i j)"),
+                        in_=flipped[:].rearrange("p s (x m) -> p s x m", x=2),
+                    )
+
         for u, (hg, pair) in enumerate(units):
-            for n0 in range(0, HW, 4):
-                flipped = tr_psum.tile([P, 4, P], F32)
-                for k in range(4):
-                    first = LEAD + CENTRE + P * (n0 + k)
-                    nc.tensor.transpose(flipped[:, k, :], skewed[:, first : first + P], identity[:])
-                nc.vector.tensor_copy(
-                    out=blocks[0:HW, :, n0 : n0 + 4], in_=flipped[0:HW].rearrange("p k r -> p r k")
-                )
-                nc.scalar.copy(
-                    out=blocks[HW:P, :, HW + n0 : HW + n0 + 4], in_=flipped[HW:P].rearrange("p k r -> p r k")
-                )
+            e6, inv_total = ready
             if u + 1 < len(units):
-                softmax_numerators(units[u + 1][0], units[u + 1][1])
-
-            y = stream.tile([P, P, SP], F32, name="y")
-            for r0 in range(0, P, Y_HEADS):
-                sums = y_psum.tile([P, Y_HEADS, Y_COLS], F32)
-                for k in range(Y_HEADS):
-                    nc.tensor.matmul(
-                        out=sums[:, k, 0 : SP + 1],
-                        lhsT=blocks[:, r0 + k, :],
-                        rhs=x3T[:, pair, P * hg + r0 + k, 0 : SP + 1],
-                        start=True,
-                        stop=True,
-                    )
-                inv_total = stream.tile([P, Y_HEADS, 1], F32, name="inv_total")
-                nc.vector.reciprocal(out=inv_total[:], in_=sums[:, :, SP : SP + 1])
-                nc.vector.tensor_tensor(
-                    out=y[:, r0 : r0 + Y_HEADS, :],
-                    in0=sums[:, :, 0:SP],
-                    in1=inv_total[:].to_broadcast([P, Y_HEADS, SP]),
-                    op=ALU.mult,
-                )
-
-            result = stream.tile([P, SP, 2, HW], F32, name="result")
-            y_cols = y[:].rearrange("p r s -> p (r s)")
-            for t0 in range(0, SP, 4):
-                back = back_psum.tile([P, 4, P], F32, name="back")
-                for k in range(4):
-                    nc.tensor.transpose(back[:, k, :], y_cols[:, P * (t0 + k) : P * (t0 + k + 1)], identity[:])
-                nc.vector.tensor_tensor(
-                    out=result[:, t0 : t0 + 4].rearrange("p t x n -> p t (x n)"),
-                    in0=back[:],
-                    in1=bias_col[:, SP * hg + t0 : SP * hg + t0 + 4].unsqueeze(2).to_broadcast([P, 4, P]),
-                    op=ALU.add,
-                )
+                ready = softmax_numerators(units[u + 1][0], units[u + 1][1])
             for xb in range(2):
+                b = 2 * pair + xb
+                x3 = x3_all[:, hg, b]
+                sums = sum_psum.tile([P, CHUNKS, P], F32)
+                for l in range(KK):
+                    dy, dx = divmod(l, WIN)
+                    i0, i1 = max(0, PAD - dy), min(SIDE, SIDE + PAD - dy)
+                    j0, j1 = max(0, PAD - dx), min(SIDE, SIDE + PAD - dx)
+                    nc.vector.tensor_tensor(
+                        out=products[:, l, :, i0:i1, j0:j1],
+                        in0=x3[:, :, i0 + dy - PAD : i1 + dy - PAD, j0 + dx - PAD : j1 + dx - PAD],
+                        in1=e6[:, xb, dy, dx, i0:i1, j0:j1].unsqueeze(1).to_broadcast([P, SP, i1 - i0, j1 - j0]),
+                        op=ALU.mult,
+                    )
+                    for c in range(CHUNKS):
+                        nc.tensor.matmul(
+                            out=sums[:, c, :],
+                            lhsT=products[:, l, CHUNK_S * c : CHUNK_S * (c + 1)].rearrange("p s i j -> p (s i j)"),
+                            rhs=identity[:],
+                            is_transpose=True,
+                            start=(l == 0 and c == 0),
+                            stop=(l == KK - 1 and c == CHUNKS - 1),
+                        )
+                sums_sb = stream.tile([P, CHUNKS, P], F32, name="sums_sb")
+                nc.scalar.copy(out=sums_sb[:], in_=sums[:])
+                back = back_psum.tile([P, SP, HW], F32)
+                for c in range(CHUNKS):
+                    nc.tensor.transpose(
+                        back[:, CHUNK_S * c : CHUNK_S * (c + 1), :].rearrange("p s n -> p (s n)"),
+                        sums_sb[:, c, :],
+                        identity[:],
+                    )
+                y = stream.tile([P, SP, HW], F32, name="y")
+                nc.vector.tensor_tensor(
+                    out=y[:], in0=back[:], in1=inv_total[:, xb, :].unsqueeze(1).to_broadcast([P, SP, HW]), op=ALU.mult
+                )
+                nc.vector.tensor_tensor(
+                    out=y[:], in0=y[:], in1=bias[:, hg, :].unsqueeze(2).to_broadcast([P, SP, HW]), op=ALU.add
+                )
                 nc.sync.dma_start(
-                    out=out[2 * pair + xb, SP * P * hg : SP * P * (hg + 1)].rearrange("(t o) i j -> o t (i j)", o=P),
-                    in_=result[:, :, xb, :],
+                    out=out[b, SP * P * hg : SP * P * (hg + 1)].rearrange("(r s) i j -> r (s i j)", s=SP),
+                    in_=y[:].rearrange("p s n -> p (s n)"),
                 )

@@ -23,8 +23,8 @@ PAD = WIN // 2
 PASSES = CIN // K_PASS
 N_TILE = 512
 HEAD_GROUPS = COUT // SP // P
-CHUNK_S = P // HW
-CHUNKS = SP // CHUNK_S
+CHUNK_ROWS = P // (SP * SIDE)
+CHUNKS = SIDE // CHUNK_ROWS
 
 FLOPS = 2 * B * HW * CIN * COUT + 2 * B * COUT * HW * KK
 
@@ -173,7 +173,7 @@ def tile_sam_pb_kernel(tc, logits, x, w3c_words, w3c_scales, b3c, out):
                     )
 
         products_pool = ctx.enter_context(tc.tile_pool(name="products", bufs=1))
-        products = products_pool.tile([P, KK, SP, SIDE, SIDE], F32)
+        products = products_pool.tile([P, KK, SIDE, SP, SIDE], F32)
         nc.vector.memset(products[:], 0.0)
 
         x3_all = keep.tile([P, HEAD_GROUPS, B, SP, SIDE, SIDE], F32)
@@ -203,32 +203,39 @@ def tile_sam_pb_kernel(tc, logits, x, w3c_words, w3c_scales, b3c, out):
                     i0, i1 = max(0, PAD - dy), min(SIDE, SIDE + PAD - dy)
                     j0, j1 = max(0, PAD - dx), min(SIDE, SIDE + PAD - dx)
                     nc.vector.tensor_tensor(
-                        out=products[:, l, :, i0:i1, j0:j1],
+                        out=products[:, l, i0:i1, :, j0:j1].rearrange("p i s j -> p s i j"),
                         in0=x3[:, :, i0 + dy - PAD : i1 + dy - PAD, j0 + dx - PAD : j1 + dx - PAD],
                         in1=e6[:, xb, dy, dx, i0:i1, j0:j1].unsqueeze(1).to_broadcast([P, SP, i1 - i0, j1 - j0]),
                         op=ALU.mult,
                     )
-                    for c in range(CHUNKS):
+                    touched = range(i0 // CHUNK_ROWS, (i1 + CHUNK_ROWS - 1) // CHUNK_ROWS)
+                    for c in touched:
                         nc.tensor.matmul(
                             out=sums[:, c, :],
-                            lhsT=products[:, l, CHUNK_S * c : CHUNK_S * (c + 1)].rearrange("p s i j -> p (s i j)"),
+                            lhsT=products[:, l, CHUNK_ROWS * c : CHUNK_ROWS * (c + 1)].rearrange("p i s j -> p (i s j)"),
                             rhs=identity[:],
                             is_transpose=True,
-                            start=(l == 0 and c == 0),
-                            stop=(l == KK - 1 and c == CHUNKS - 1),
+                            start=(l == 0 and c == touched[0]),
+                            stop=(l == KK - 1 and c == touched[-1]),
                         )
                 sums_sb = stream.tile([P, CHUNKS, P], F32, name="sums_sb")
                 nc.scalar.copy(out=sums_sb[:], in_=sums[:])
-                back = back_psum.tile([P, SP, HW], F32)
+                back = back_psum.tile([P, SIDE, SP, SIDE], F32)
                 for c in range(CHUNKS):
                     nc.tensor.transpose(
-                        back[:, CHUNK_S * c : CHUNK_S * (c + 1), :].rearrange("p s n -> p (s n)"),
+                        back[:, CHUNK_ROWS * c : CHUNK_ROWS * (c + 1)].rearrange("p i s j -> p (i s j)"),
                         sums_sb[:, c, :],
                         identity[:],
                     )
                 y = stream.tile([P, SP, HW], F32, name="y")
                 nc.vector.tensor_tensor(
-                    out=y[:], in0=back[:], in1=inv_total[:, xb, :].unsqueeze(1).to_broadcast([P, SP, HW]), op=ALU.mult
+                    out=y[:].rearrange("p s (i j) -> p s i j", i=SIDE),
+                    in0=back[:].rearrange("p i s j -> p s i j"),
+                    in1=inv_total[:, xb, :]
+                    .rearrange("p (i j) -> p i j", i=SIDE)
+                    .unsqueeze(1)
+                    .to_broadcast([P, SP, SIDE, SIDE]),
+                    op=ALU.mult,
                 )
                 nc.vector.tensor_tensor(
                     out=y[:], in0=y[:], in1=bias[:, hg, :].unsqueeze(2).to_broadcast([P, SP, HW]), op=ALU.add

@@ -77,36 +77,36 @@ def tile_sam_pb_kernel(tc, logits, x, w3c_words, w3c_scales, b3c, out):
                 out=top[:, :, 0:1, :], in0=top[:, :, 0:1, :], in1=lg[:, :, KK // 2 : KK // 2 + 1, :], op=ALU.max
             )
             e = stream.tile([P, 2, KK, HW], F32, name="e")
-            nc.gpsimd.tensor_tensor(
+            nc.vector.tensor_tensor(
                 out=e[:], in0=lg[:], in1=top[:, :, 0:1, :].to_broadcast([P, 2, KK, HW]), op=ALU.subtract
             )
             nc.scalar.activation(out=e[:], in_=e[:], func=ACT.Exp)
             part = keep.tile([P, 2, KK // 2, HW], F32, name="part")
-            nc.gpsimd.tensor_tensor(
+            nc.vector.tensor_tensor(
                 out=part[:], in0=e[:, :, 0 : KK // 2, :], in1=e[:, :, KK // 2 + 1 : KK, :], op=ALU.add
             )
             rows = KK // 2
             while rows > 1:
                 half = rows // 2
-                nc.gpsimd.tensor_tensor(
+                nc.vector.tensor_tensor(
                     out=part[:, :, 0:half, :],
                     in0=part[:, :, 0:half, :],
                     in1=part[:, :, rows - half : rows, :],
                     op=ALU.add,
                 )
                 rows = rows - half
-            nc.gpsimd.tensor_tensor(
+            nc.vector.tensor_tensor(
                 out=part[:, :, 0:1, :], in0=part[:, :, 0:1, :], in1=e[:, :, KK // 2 : KK // 2 + 1, :], op=ALU.add
             )
             inv_total = stream.tile([P, 2, HW], F32, name="inv_total")
             nc.vector.reciprocal(out=inv_total[:], in_=part[:, :, 0, :])
             e6 = e[:].rearrange("p x (dy dx) (i j) -> p x dy dx i j", dy=WIN, i=SIDE)
             for i, src, dst in folds:
-                nc.gpsimd.tensor_tensor(
+                nc.vector.tensor_tensor(
                     out=e6[:, :, dst, :, i, :], in0=e6[:, :, dst, :, i, :], in1=e6[:, :, src, :, i, :], op=ALU.add
                 )
             for j, src, dst in folds:
-                nc.gpsimd.tensor_tensor(
+                nc.vector.tensor_tensor(
                     out=e6[:, :, :, dst, :, j], in0=e6[:, :, :, dst, :, j], in1=e6[:, :, :, src, :, j], op=ALU.add
                 )
             return e6, inv_total

@@ -23,21 +23,28 @@ PAD = WIN // 2
 PASSES = CIN // K_PASS
 N_TILE = 512
 HEAD_GROUPS = COUT // SP // P
-CHUNK_ROWS = P // (SP * SIDE)
-CHUNKS = SIDE // CHUNK_ROWS
+PAIRS = B // 2
+PADDED = SIDE + 2 * PAD
+BANK_ROWS = N_TILE // P
 
 FLOPS = 2 * B * HW * CIN * COUT + 2 * B * COUT * HW * KK
 
 
+def mirror(u):
+    if u < 0:
+        return -u
+    if u > SIDE - 1:
+        return 2 * (SIDE - 1) - u
+    return u
+
+
 def outside_offsets():
     found = []
-    for pos in range(SIDE):
-        for off in range(WIN):
-            u = pos + off - PAD
-            if u < 0:
-                found.append((pos, off, -u - pos + PAD))
-            elif u > SIDE - 1:
-                found.append((pos, off, 2 * (SIDE - 1) - u - pos + PAD))
+    for i in range(SIDE):
+        for dy in range(WIN):
+            u = i + dy - PAD
+            if mirror(u) != u:
+                found.append((i, dy, mirror(u) - i + PAD))
     return found
 
 
@@ -47,10 +54,11 @@ def tile_sam_pb_kernel(tc, logits, x, w3c_words, w3c_scales, b3c, out):
     with ExitStack() as ctx:
         keep = ctx.enter_context(tc.tile_pool(name="keep", bufs=1))
         stream = ctx.enter_context(tc.tile_pool(name="stream", bufs=2))
-        mx_psum = ctx.enter_context(tc.psum_pool(name="mx_psum", bufs=2))
-        x3_psum = ctx.enter_context(tc.psum_pool(name="x3_psum", bufs=2))
+        prod_pool = ctx.enter_context(tc.tile_pool(name="prod", bufs=6))
+        front_psum = ctx.enter_context(tc.psum_pool(name="front_psum", bufs=2))
+        small_psum = ctx.enter_context(tc.psum_pool(name="small_psum", bufs=1))
+        back_psum = ctx.enter_context(tc.psum_pool(name="back_psum", bufs=1))
         sum_psum = ctx.enter_context(tc.psum_pool(name="sum_psum", bufs=2))
-        back_psum = ctx.enter_context(tc.psum_pool(name="back_psum", bufs=2))
 
         identity = keep.tile([P, P], F32)
         make_identity(nc, identity[:])
@@ -76,42 +84,36 @@ def tile_sam_pb_kernel(tc, logits, x, w3c_words, w3c_scales, b3c, out):
             nc.vector.tensor_tensor(
                 out=top[:, :, 0:1, :], in0=top[:, :, 0:1, :], in1=lg[:, :, KK // 2 : KK // 2 + 1, :], op=ALU.max
             )
-            e = stream.tile([P, 2, KK, HW], F32, name="e")
+            e = stream.tile([P, KK, 2, HW], F32, name="e")
             nc.vector.tensor_tensor(
-                out=e[:], in0=lg[:], in1=top[:, :, 0:1, :].to_broadcast([P, 2, KK, HW]), op=ALU.subtract
+                out=e[:].rearrange("p l x n -> p x l n"),
+                in0=lg[:],
+                in1=top[:, :, 0:1, :].to_broadcast([P, 2, KK, HW]),
+                op=ALU.subtract,
             )
             nc.scalar.activation(out=e[:], in_=e[:], func=ACT.Exp)
-            part = keep.tile([P, 2, KK // 2, HW], F32, name="part")
-            nc.vector.tensor_tensor(
-                out=part[:], in0=e[:, :, 0 : KK // 2, :], in1=e[:, :, KK // 2 + 1 : KK, :], op=ALU.add
-            )
-            rows = KK // 2
-            while rows > 1:
-                half = rows // 2
-                nc.vector.tensor_tensor(
-                    out=part[:, :, 0:half, :],
-                    in0=part[:, :, 0:half, :],
-                    in1=part[:, :, rows - half : rows, :],
-                    op=ALU.add,
+            total_t = small_psum.tile([P, P], F32, name="small")
+            for l in range(KK):
+                nc.tensor.matmul(
+                    out=total_t[:],
+                    lhsT=e[:, l].rearrange("p x n -> p (x n)"),
+                    rhs=identity[:],
+                    is_transpose=True,
+                    start=(l == 0),
+                    stop=(l == KK - 1),
                 )
-                rows = rows - half
-            nc.vector.tensor_tensor(
-                out=part[:, :, 0:1, :], in0=part[:, :, 0:1, :], in1=e[:, :, KK // 2 : KK // 2 + 1, :], op=ALU.add
-            )
+            total_sb = stream.tile([P, P], F32, name="total_sb")
+            nc.scalar.copy(out=total_sb[:], in_=total_t[:])
+            total = small_psum.tile([P, P], F32, name="small")
+            nc.tensor.transpose(total[:], total_sb[:], identity[:])
             inv_total = stream.tile([P, 2, HW], F32, name="inv_total")
-            nc.vector.reciprocal(out=inv_total[:], in_=part[:, :, 0, :])
-            e6 = e[:].rearrange("p x (dy dx) (i j) -> p x dy dx i j", dy=WIN, i=SIDE)
+            nc.vector.reciprocal(out=inv_total[:].rearrange("p x n -> p (x n)"), in_=total[:])
+            by_row = e[:].rearrange("p (dy dx) x (i j) -> p dy i dx x j", dy=WIN, i=SIDE)
             for i, src, dst in folds:
-                nc.vector.tensor_tensor(
-                    out=e6[:, :, dst, :, i, :], in0=e6[:, :, dst, :, i, :], in1=e6[:, :, src, :, i, :], op=ALU.add
-                )
-            for j, src, dst in folds:
-                nc.vector.tensor_tensor(
-                    out=e6[:, :, :, dst, :, j], in0=e6[:, :, :, dst, :, j], in1=e6[:, :, :, src, :, j], op=ALU.add
-                )
-            return e6, inv_total
+                nc.vector.tensor_tensor(out=by_row[:, dst, i], in0=by_row[:, dst, i], in1=by_row[:, src, i], op=ALU.add)
+            return e, inv_total
 
-        units = [(hg, pair) for hg in range(HEAD_GROUPS) for pair in range(B // 2)]
+        units = [(hg, pair) for hg in range(HEAD_GROUPS) for pair in range(PAIRS)]
         ready = softmax_numerators(units[0][0], units[0][1])
 
         bias_bf = keep.tile([P, HEAD_GROUPS, SP], BF16)
@@ -119,7 +121,7 @@ def tile_sam_pb_kernel(tc, logits, x, w3c_words, w3c_scales, b3c, out):
         bias = keep.tile([P, HEAD_GROUPS, SP], F32)
         nc.vector.tensor_copy(out=bias[:], in_=bias_bf[:])
 
-        x3T = keep.tile([P, B // 2, SP, COUT // SP], F32)
+        x3T = keep.tile([P, PAIRS, SP, COUT // SP], F32)
         with tc.tile_pool(name="front", bufs=1) as front:
             x_raw = front.tile([P, B, PASSES, PACK, HW], BF16)
             nc.sync.dma_start(
@@ -153,10 +155,10 @@ def tile_sam_pb_kernel(tc, logits, x, w3c_words, w3c_scales, b3c, out):
                 nc.sync.dma_start(out=w_words[:, g, :].bitcast(I32), in_=w3c_words[g].bitcast(I32))
 
             heads_per_tile = N_TILE // SP
-            for pair in range(B // 2):
+            for pair in range(PAIRS):
                 cols = slice(P * pair, P * (pair + 1))
                 for ot in range(COUT // N_TILE):
-                    acc = mx_psum.tile([P, N_TILE], F32)
+                    acc = front_psum.tile([P, N_TILE], F32, name="front")
                     for g in range(PASSES):
                         nc.tensor.matmul_mx(
                             out=acc[:],
@@ -172,75 +174,85 @@ def tile_sam_pb_kernel(tc, logits, x, w3c_words, w3c_scales, b3c, out):
                         in_=acc[:].rearrange("p (h s) -> p s h", s=SP),
                     )
 
-        products_pool = ctx.enter_context(tc.tile_pool(name="products", bufs=1))
-        products = products_pool.tile([P, KK, SIDE, SP, SIDE], F32)
-        nc.vector.memset(products[:], 0.0)
-
-        x3_all = keep.tile([P, HEAD_GROUPS, B, SP, SIDE, SIDE], F32)
-        for pair in range(B // 2):
+        x3 = keep.tile([P, HEAD_GROUPS, B, SIDE, PADDED, SP], F32)
+        for pair in range(PAIRS):
             for hg in range(HEAD_GROUPS):
                 for s0 in range(0, SP, 4):
-                    flipped = x3_psum.tile([P, 4, P], F32)
+                    flipped = front_psum.tile([P, 4, 2, HW], F32, name="front")
                     for k in range(4):
                         nc.tensor.transpose(
-                            flipped[:, k, :], x3T[:, pair, s0 + k, P * hg : P * (hg + 1)], identity[:]
+                            flipped[:, k].rearrange("p x m -> p (x m)"),
+                            x3T[:, pair, s0 + k, P * hg : P * (hg + 1)],
+                            identity[:],
                         )
-                    nc.scalar.copy(
-                        out=x3_all[:, hg, 2 * pair : 2 * pair + 2, s0 : s0 + 4].rearrange("p x s i j -> p s x (i j)"),
-                        in_=flipped[:].rearrange("p s (x m) -> p s x m", x=2),
-                    )
+                    for xb in range(2):
+                        nc.scalar.copy(
+                            out=x3[:, hg, 2 * pair + xb, :, PAD : PAD + SIDE, s0 : s0 + 4],
+                            in_=flipped[:, :, xb, :].rearrange("p s (i j) -> p i j s", i=SIDE),
+                        )
+        image_rows = x3[:].rearrange("p g b i c s -> p (g b i) c s")
+        for c in [c for c in range(PADDED) if mirror(c - PAD) != c - PAD]:
+            nc.scalar.copy(out=image_rows[:, :, c, :], in_=image_rows[:, :, mirror(c - PAD) + PAD, :])
 
         for u, (hg, pair) in enumerate(units):
-            e6, inv_total = ready
+            e, inv_total = ready
             if u + 1 < len(units):
                 ready = softmax_numerators(units[u + 1][0], units[u + 1][1])
-            for xb in range(2):
-                b = 2 * pair + xb
-                x3 = x3_all[:, hg, b]
-                sums = sum_psum.tile([P, CHUNKS, P], F32)
-                for l in range(KK):
-                    dy, dx = divmod(l, WIN)
-                    i0, i1 = max(0, PAD - dy), min(SIDE, SIDE + PAD - dy)
-                    j0, j1 = max(0, PAD - dx), min(SIDE, SIDE + PAD - dx)
-                    nc.vector.tensor_tensor(
-                        out=products[:, l, i0:i1, :, j0:j1].rearrange("p i s j -> p s i j"),
-                        in0=x3[:, :, i0 + dy - PAD : i1 + dy - PAD, j0 + dx - PAD : j1 + dx - PAD],
-                        in1=e6[:, xb, dy, dx, i0:i1, j0:j1].unsqueeze(1).to_broadcast([P, SP, i1 - i0, j1 - j0]),
-                        op=ALU.mult,
-                    )
-                    touched = range(i0 // CHUNK_ROWS, (i1 + CHUNK_ROWS - 1) // CHUNK_ROWS)
-                    for c in touched:
-                        nc.tensor.matmul(
-                            out=sums[:, c, :],
-                            lhsT=products[:, l, CHUNK_ROWS * c : CHUNK_ROWS * (c + 1)].rearrange("p i s j -> p (i s j)"),
-                            rhs=identity[:],
-                            is_transpose=True,
-                            start=(l == 0 and c == touched[0]),
-                            stop=(l == KK - 1 and c == touched[-1]),
-                        )
-                sums_sb = stream.tile([P, CHUNKS, P], F32, name="sums_sb")
-                nc.scalar.copy(out=sums_sb[:], in_=sums[:])
-                back = back_psum.tile([P, SIDE, SP, SIDE], F32)
-                for c in range(CHUNKS):
-                    nc.tensor.transpose(
-                        back[:, CHUNK_ROWS * c : CHUNK_ROWS * (c + 1)].rearrange("p i s j -> p (i s j)"),
-                        sums_sb[:, c, :],
-                        identity[:],
-                    )
-                y = stream.tile([P, SP, HW], F32, name="y")
+            sums = [
+                sum_psum.tile([P, BANK_ROWS, P], F32, name="sums%d" % half) for half in range(SIDE // BANK_ROWS)
+            ]
+            for l in range(KK):
+                dy, dx = divmod(l, WIN)
+                i0, i1 = max(0, PAD - dy), min(SIDE, SIDE + PAD - dy)
+                prod = prod_pool.tile([P, SIDE, 2, SIDE, SP], F32, name="prod")
                 nc.vector.tensor_tensor(
-                    out=y[:].rearrange("p s (i j) -> p s i j", i=SIDE),
-                    in0=back[:].rearrange("p i s j -> p s i j"),
-                    in1=inv_total[:, xb, :]
-                    .rearrange("p (i j) -> p i j", i=SIDE)
-                    .unsqueeze(1)
-                    .to_broadcast([P, SP, SIDE, SIDE]),
+                    out=prod[:, i0:i1].rearrange("p i x j s -> p x i j s"),
+                    in0=x3[:, hg, 2 * pair : 2 * pair + 2, i0 + dy - PAD : i1 + dy - PAD, dx : dx + SIDE, :],
+                    in1=e[:, l, :, SIDE * i0 : SIDE * i1]
+                    .rearrange("p x (i j) -> p x i j", j=SIDE)
+                    .unsqueeze(4)
+                    .to_broadcast([P, 2, i1 - i0, SIDE, SP]),
                     op=ALU.mult,
                 )
-                nc.vector.tensor_tensor(
-                    out=y[:], in0=y[:], in1=bias[:, hg, :].unsqueeze(2).to_broadcast([P, SP, HW]), op=ALU.add
-                )
+                for i in range(i0, i1):
+                    half = i // BANK_ROWS
+                    first_in_bank = max(i0, BANK_ROWS * half)
+                    last_in_bank = min(i1, BANK_ROWS * (half + 1)) - 1
+                    nc.tensor.matmul(
+                        out=sums[half][:, i % BANK_ROWS, :],
+                        lhsT=prod[:, i].rearrange("p x j s -> p (x j s)"),
+                        rhs=identity[:],
+                        is_transpose=True,
+                        start=(l == 0 and i == first_in_bank),
+                        stop=(l == KK - 1 and i == last_in_bank),
+                    )
+
+            y = stream.tile([P, 2, SP, HW], F32, name="y")
+            for half in range(SIDE // BANK_ROWS):
+                sums_sb = stream.tile([P, BANK_ROWS, P], F32, name="sums_sb")
+                nc.scalar.copy(out=sums_sb[:], in_=sums[half][:])
+                back = back_psum.tile([P, BANK_ROWS, 2, SIDE, SP], F32)
+                for k in range(BANK_ROWS):
+                    nc.tensor.transpose(back[:, k].rearrange("p x j s -> p (x j s)"), sums_sb[:, k, :], identity[:])
+                positions = slice(SIDE * BANK_ROWS * half, SIDE * BANK_ROWS * (half + 1))
+                for xb in range(2):
+                    nc.vector.tensor_tensor(
+                        out=y[:, xb, :, positions].rearrange("p s (i j) -> p s i j", j=SIDE),
+                        in0=back[:, :, xb].rearrange("p i j s -> p s i j"),
+                        in1=inv_total[:, xb, positions]
+                        .rearrange("p (i j) -> p i j", j=SIDE)
+                        .unsqueeze(1)
+                        .to_broadcast([P, SP, BANK_ROWS, SIDE]),
+                        op=ALU.mult,
+                    )
+            nc.vector.tensor_tensor(
+                out=y[:],
+                in0=y[:],
+                in1=bias[:, hg, :].unsqueeze(1).unsqueeze(3).to_broadcast([P, 2, SP, HW]),
+                op=ALU.add,
+            )
+            for xb in range(2):
                 nc.sync.dma_start(
-                    out=out[b, SP * P * hg : SP * P * (hg + 1)].rearrange("(r s) i j -> r (s i j)", s=SP),
-                    in_=y[:].rearrange("p s n -> p (s n)"),
+                    out=out[2 * pair + xb, SP * P * hg : SP * P * (hg + 1)].rearrange("(r s) i j -> r (s i j)", s=SP),
+                    in_=y[:, xb].rearrange("p s n -> p (s n)"),
                 )

@@ -26,6 +26,7 @@ HEAD_GROUPS = COUT // SP // P
 PAIRS = B // 2
 PADDED = SIDE + 2 * PAD
 BANK_ROWS = N_TILE // P
+PITCH = 52
 
 FLOPS = 2 * B * HW * CIN * COUT + 2 * B * COUT * HW * KK
 
@@ -56,7 +57,6 @@ def tile_sam_pb_kernel(tc, logits, x, w3c_words, w3c_scales, b3c, out):
         stream = ctx.enter_context(tc.tile_pool(name="stream", bufs=2))
         prod_pool = ctx.enter_context(tc.tile_pool(name="prod", bufs=6))
         front_psum = ctx.enter_context(tc.psum_pool(name="front_psum", bufs=2))
-        small_psum = ctx.enter_context(tc.psum_pool(name="small_psum", bufs=1))
         back_psum = ctx.enter_context(tc.psum_pool(name="back_psum", bufs=1))
         sum_psum = ctx.enter_context(tc.psum_pool(name="sum_psum", bufs=2))
 
@@ -84,33 +84,30 @@ def tile_sam_pb_kernel(tc, logits, x, w3c_words, w3c_scales, b3c, out):
             nc.vector.tensor_tensor(
                 out=top[:, :, 0:1, :], in0=top[:, :, 0:1, :], in1=lg[:, :, KK // 2 : KK // 2 + 1, :], op=ALU.max
             )
-            e = stream.tile([P, KK, 2, HW], F32, name="e")
-            nc.vector.tensor_tensor(
-                out=e[:].rearrange("p l x n -> p x l n"),
-                in0=lg[:],
-                in1=top[:, :, 0:1, :].to_broadcast([P, 2, KK, HW]),
-                op=ALU.subtract,
-            )
-            nc.scalar.activation(out=e[:], in_=e[:], func=ACT.Exp)
-            total_t = small_psum.tile([P, P], F32, name="small")
-            for l in range(KK):
-                nc.tensor.matmul(
-                    out=total_t[:],
-                    lhsT=e[:, l].rearrange("p x n -> p (x n)"),
-                    rhs=identity[:],
-                    is_transpose=True,
-                    start=(l == 0),
-                    stop=(l == KK - 1),
-                )
-            total_sb = stream.tile([P, P], F32, name="total_sb")
-            nc.scalar.copy(out=total_sb[:], in_=total_t[:])
-            total = small_psum.tile([P, P], F32, name="small")
-            nc.tensor.transpose(total[:], total_sb[:], identity[:])
+            minus_top = stream.tile([P, 2, HW], F32, name="minus_top")
+            nc.vector.tensor_scalar_mul(out=minus_top[:], in0=top[:, :, 0, :], scalar1=-1.0)
+            e = stream.tile([P, 2, HW, PITCH], F32, name="e")
+            total = stream.tile([P, 2, HW], F32, name="total")
+            for xb in range(2):
+                for n in range(HW):
+                    nc.scalar.activation(
+                        out=e[:, xb, n, 0:KK],
+                        in_=lg[:, xb, :, n],
+                        func=ACT.Exp,
+                        bias=minus_top[:, xb, n : n + 1],
+                        scale=1.0,
+                        accum_out=total[:, xb, n : n + 1],
+                    )
             inv_total = stream.tile([P, 2, HW], F32, name="inv_total")
-            nc.vector.reciprocal(out=inv_total[:].rearrange("p x n -> p (x n)"), in_=total[:])
-            by_row = e[:].rearrange("p (dy dx) x (i j) -> p dy i dx x j", dy=WIN, i=SIDE)
+            nc.vector.reciprocal(out=inv_total[:], in_=total[:])
+            by_row = e[:].rearrange("p x (i j) l -> p x i j l", i=SIDE)
             for i, src, dst in folds:
-                nc.vector.tensor_tensor(out=by_row[:, dst, i], in0=by_row[:, dst, i], in1=by_row[:, src, i], op=ALU.add)
+                nc.vector.tensor_tensor(
+                    out=by_row[:, :, i, :, WIN * dst : WIN * (dst + 1)],
+                    in0=by_row[:, :, i, :, WIN * dst : WIN * (dst + 1)],
+                    in1=by_row[:, :, i, :, WIN * src : WIN * (src + 1)],
+                    op=ALU.add,
+                )
             return e, inv_total
 
         units = [(hg, pair) for hg in range(HEAD_GROUPS) for pair in range(PAIRS)]
@@ -208,7 +205,7 @@ def tile_sam_pb_kernel(tc, logits, x, w3c_words, w3c_scales, b3c, out):
                 nc.vector.tensor_tensor(
                     out=prod[:, i0:i1].rearrange("p i x j s -> p x i j s"),
                     in0=x3[:, hg, 2 * pair : 2 * pair + 2, i0 + dy - PAD : i1 + dy - PAD, dx : dx + SIDE, :],
-                    in1=e[:, l, :, SIDE * i0 : SIDE * i1]
+                    in1=e[:, :, SIDE * i0 : SIDE * i1, l]
                     .rearrange("p x (i j) -> p x i j", j=SIDE)
                     .unsqueeze(4)
                     .to_broadcast([P, 2, i1 - i0, SIDE, SP]),

@@ -24,9 +24,11 @@ PASSES = CIN // K_PASS
 N_TILE = 512
 HEAD_GROUPS = COUT // SP // P
 PAIRS = B // 2
-PADDED = SIDE + 2 * PAD
 BANK_ROWS = N_TILE // P
+BANKS = SIDE // BANK_ROWS
 PITCH = 52
+SH = SP // 2
+PROD_BUFS = 2
 
 FLOPS = 2 * B * HW * CIN * COUT + 2 * B * COUT * HW * KK
 
@@ -49,98 +51,114 @@ def outside_offsets():
     return found
 
 
+def inside(d):
+    return max(0, PAD - d), min(SIDE, SIDE + PAD - d)
+
+
 def tile_sam_pb_kernel(tc, logits, x, w3c_words, w3c_scales, b3c, out):
     nc = tc.nc
     folds = outside_offsets()
+    units = [(hg, pair) for hg in range(HEAD_GROUPS) for pair in range(PAIRS)]
     with ExitStack() as ctx:
         keep = ctx.enter_context(tc.tile_pool(name="keep", bufs=1))
         stream = ctx.enter_context(tc.tile_pool(name="stream", bufs=2))
-        prod_pool = ctx.enter_context(tc.tile_pool(name="prod", bufs=6))
         front_psum = ctx.enter_context(tc.psum_pool(name="front_psum", bufs=2))
-        back_psum = ctx.enter_context(tc.psum_pool(name="back_psum", bufs=1))
-        sum_psum = ctx.enter_context(tc.psum_pool(name="sum_psum", bufs=2))
+        x3_psum = ctx.enter_context(tc.psum_pool(name="x3_psum", bufs=2))
+        sum_psum = ctx.enter_context(tc.psum_pool(name="sum_psum", bufs=1))
 
         identity = keep.tile([P, P], F32)
         make_identity(nc, identity[:])
 
-        def softmax_numerators(hg, pair):
-            lg = stream.tile([P, 2, KK, HW], BF16, name="lg")
-            for xb in range(2):
-                nc.sync.dma_start(out=lg[:, xb], in_=logits[2 * pair + xb, P * hg : P * (hg + 1)])
-            top = keep.tile([P, 2, KK // 2, HW], BF16, name="top")
+        prod_tiles = {}
+        for dx in range(WIN):
+            j0, j1 = inside(dx)
+            for k in range(PROD_BUFS):
+                t = keep.tile([P, SIDE, SIDE, 2, SP], F32, name="prod_%d_%d" % (dx, k))
+                if j0 > 0:
+                    nc.gpsimd.memset(t[:, :, 0:j0, :, :], 0.0)
+                if j1 < SIDE:
+                    nc.gpsimd.memset(t[:, :, j1:SIDE, :, :], 0.0)
+                prod_tiles[(dx, k)] = t
+
+        lg = [keep.tile([P, 2, KK, HW], BF16, name="lg%d" % u) for u in range(len(units))]
+        minus_top = [keep.tile([P, HW, 2], F32, name="minus_top%d" % u) for u in range(len(units))]
+
+        def load_logits(u, xb):
+            hg, pair = units[u]
+            nc.sync.dma_start(out=lg[u][:, xb], in_=logits[2 * pair + xb, P * hg : P * (hg + 1)])
+
+        def maximum(u, xb):
+            top = stream.tile([P, KK // 2, HW], BF16, name="top")
             nc.vector.tensor_tensor(
-                out=top[:], in0=lg[:, :, 0 : KK // 2, :], in1=lg[:, :, KK // 2 + 1 : KK, :], op=ALU.max
+                out=top[:], in0=lg[u][:, xb, 0 : KK // 2, :], in1=lg[u][:, xb, KK // 2 + 1 : KK, :], op=ALU.max
             )
             rows = KK // 2
             while rows > 1:
                 half = rows // 2
                 nc.vector.tensor_tensor(
-                    out=top[:, :, 0:half, :],
-                    in0=top[:, :, 0:half, :],
-                    in1=top[:, :, rows - half : rows, :],
-                    op=ALU.max,
+                    out=top[:, 0:half, :], in0=top[:, 0:half, :], in1=top[:, rows - half : rows, :], op=ALU.max
                 )
                 rows = rows - half
             nc.vector.tensor_tensor(
-                out=top[:, :, 0:1, :], in0=top[:, :, 0:1, :], in1=lg[:, :, KK // 2 : KK // 2 + 1, :], op=ALU.max
+                out=top[:, 0:1, :], in0=top[:, 0:1, :], in1=lg[u][:, xb, KK // 2 : KK // 2 + 1, :], op=ALU.max
             )
-            minus_top = stream.tile([P, 2, HW], F32, name="minus_top")
-            nc.vector.tensor_scalar_mul(out=minus_top[:], in0=top[:, :, 0, :], scalar1=-1.0)
-            e = stream.tile([P, 2, HW, PITCH], F32, name="e")
-            total = stream.tile([P, 2, HW], F32, name="total")
-            for xb in range(2):
-                for n in range(HW):
+            nc.vector.tensor_scalar_mul(out=minus_top[u][:, :, xb], in0=top[:, 0, :], scalar1=-1.0)
+
+        def numerators(u):
+            e = stream.tile([P, HW, 2, PITCH], F32, name="e")
+            total = stream.tile([P, HW, 2], F32, name="total")
+            for n in range(HW):
+                for xb in range(2):
                     nc.scalar.activation(
-                        out=e[:, xb, n, 0:KK],
-                        in_=lg[:, xb, :, n],
+                        out=e[:, n, xb, 0:KK],
+                        in_=lg[u][:, xb, :, n],
                         func=ACT.Exp,
-                        bias=minus_top[:, xb, n : n + 1],
+                        bias=minus_top[u][:, n, xb : xb + 1],
                         scale=1.0,
-                        accum_out=total[:, xb, n : n + 1],
+                        accum_out=total[:, n, xb : xb + 1],
                     )
-            inv_total = stream.tile([P, 2, HW], F32, name="inv_total")
-            nc.vector.reciprocal(out=inv_total[:], in_=total[:])
-            by_row = e[:].rearrange("p x (i j) l -> p x i j l", i=SIDE)
+            return e, total
+
+        def fold(e, total):
+            view = e[:, :, :, 0:KK].rearrange("p (i j) x (dy dx) -> p i j x dy dx", i=SIDE, dy=WIN)
             for i, src, dst in folds:
-                nc.vector.tensor_tensor(
-                    out=by_row[:, :, i, :, WIN * dst : WIN * (dst + 1)],
-                    in0=by_row[:, :, i, :, WIN * dst : WIN * (dst + 1)],
-                    in1=by_row[:, :, i, :, WIN * src : WIN * (src + 1)],
-                    op=ALU.add,
+                nc.gpsimd.tensor_tensor(
+                    out=view[:, i, :, :, dst, :], in0=view[:, i, :, :, dst, :], in1=view[:, i, :, :, src, :], op=ALU.add
                 )
-            return e, inv_total
-
-        units = [(hg, pair) for hg in range(HEAD_GROUPS) for pair in range(PAIRS)]
-        ready = softmax_numerators(units[0][0], units[0][1])
-
-        bias_bf = keep.tile([P, HEAD_GROUPS, SP], BF16)
-        nc.scalar.dma_start(out=bias_bf[:], in_=b3c.rearrange("(g r s) -> r g s", g=HEAD_GROUPS, r=P))
-        bias = keep.tile([P, HEAD_GROUPS, SP], F32)
-        nc.vector.tensor_copy(out=bias[:], in_=bias_bf[:])
+            for j, src, dst in folds:
+                nc.gpsimd.tensor_tensor(
+                    out=view[:, :, j, :, :, dst], in0=view[:, :, j, :, :, dst], in1=view[:, :, j, :, :, src], op=ALU.add
+                )
+            inv_total = stream.tile([P, HW, 2], F32, name="inv_total")
+            nc.vector.reciprocal(out=inv_total[:], in_=total[:])
+            return inv_total
 
         x3T = keep.tile([P, PAIRS, SP, COUT // SP], F32)
+
+        def heads_to_partitions(u):
+            hg, pair = units[u]
+            banks = [x3_psum.tile([P, SIDE, SIDE, 2, SH], F32, name="x3_%d" % h) for h in range(SP // SH)]
+            for s in range(SP):
+                nc.tensor.transpose(
+                    banks[s // SH][:].rearrange("p i j x s -> p (i j x) s")[:, :, s % SH],
+                    x3T[:, pair, s, P * hg : P * (hg + 1)],
+                    identity[:],
+                )
+            return banks
+
+        bias_bf = keep.tile([P, HEAD_GROUPS, SP], BF16)
+        bias = keep.tile([P, HEAD_GROUPS, SP], F32)
+
         with tc.tile_pool(name="front", bufs=1) as front:
+            w_scales = front.tile([P, PASSES, COUT], U8, align_bytes=64)
+            nc.vector.memset(w_scales[:].rearrange("p g n -> p (g n)").bitcast(I32), 0)
+
+            load_logits(0, 0)
             x_raw = front.tile([P, B, PASSES, PACK, HW], BF16)
             nc.sync.dma_start(
                 out=x_raw[:], in_=x.rearrange("b (g p t) i j -> p b g t (i j)", g=PASSES, p=P, t=PACK)
             )
-            x_grouped = front.tile([P, PASSES, B * HW, PACK], BF16, align_bytes=64)
-            x_codes = front.tile([P, PASSES, B * HW], U32, align_bytes=64)
-            x_scales = front.tile([P, PASSES, B * HW], U8, align_bytes=64)
-            for g in range(PASSES):
-                nc.vector.tensor_copy(
-                    out=x_grouped[:, g].rearrange("p (b n) t -> p b n t", b=B),
-                    in_=x_raw[:, :, g].rearrange("p b t n -> p b n t"),
-                )
-            for g in range(PASSES):
-                nc.vector.quantize_mx(
-                    out=x_codes[:, g, :].bitcast(FP8X4),
-                    scales=x_scales[:, g, :],
-                    in_=x_grouped[:, g].rearrange("p c t -> p (c t)"),
-                )
-
-            w_scales = front.tile([P, PASSES, COUT], U8, align_bytes=64)
-            nc.vector.memset(w_scales[:].rearrange("p g n -> p (g n)").bitcast(I32), 0)
+            load_logits(0, 1)
             for half in range(2):
                 for r in range(4):
                     nc.sync.dma_start(
@@ -148,13 +166,43 @@ def tile_sam_pb_kernel(tc, logits, x, w3c_words, w3c_scales, b3c, out):
                         in_=w3c_scales[:, 4 * half + r : 16 : 8, :].rearrange("g q n -> q g n").bitcast(I32),
                     )
             w_words = front.tile([P, PASSES, 2 * COUT], U8, align_bytes=64)
+            for hg in range(HEAD_GROUPS):
+                for g in range(PASSES):
+                    nc.sync.dma_start(
+                        out=w_words[:, g, COUT * hg : COUT * (hg + 1)].bitcast(I32),
+                        in_=w3c_words[g][:, COUT * hg : COUT * (hg + 1)].bitcast(I32),
+                    )
+                for xb in range(2):
+                    load_logits(1 + hg, xb)
+            for xb in range(2):
+                load_logits(3, xb)
+            nc.scalar.dma_start(out=bias_bf[:], in_=b3c.rearrange("(g r s) -> r g s", g=HEAD_GROUPS, r=P))
+
+            maximum(0, 0)
+            maximum(0, 1)
+            ready = numerators(0)
+
+            x_grouped = front.tile([P, PASSES, B * HW, PACK], BF16, align_bytes=64)
+            x_codes = front.tile([P, PASSES, B * HW], U32, align_bytes=64)
+            x_scales = front.tile([P, PASSES, B * HW], U8, align_bytes=64)
             for g in range(PASSES):
-                nc.sync.dma_start(out=w_words[:, g, :].bitcast(I32), in_=w3c_words[g].bitcast(I32))
+                for pair in range(PAIRS):
+                    nc.vector.tensor_copy(
+                        out=x_grouped[:, g, P * pair : P * (pair + 1), :].rearrange("p (n x) t -> p n x t", x=2),
+                        in_=x_raw[:, 2 * pair : 2 * pair + 2, g].rearrange("p x t n -> p n x t"),
+                    )
+            for g in range(PASSES):
+                nc.vector.quantize_mx(
+                    out=x_codes[:, g, :].bitcast(FP8X4),
+                    scales=x_scales[:, g, :],
+                    in_=x_grouped[:, g].rearrange("p c t -> p (c t)"),
+                )
+            nc.vector.tensor_copy(out=bias[:], in_=bias_bf[:])
 
             heads_per_tile = N_TILE // SP
-            for pair in range(PAIRS):
+            for u, (hg, pair) in enumerate(units):
                 cols = slice(P * pair, P * (pair + 1))
-                for ot in range(COUT // N_TILE):
+                for ot in range(2 * hg, 2 * hg + 2):
                     acc = front_psum.tile([P, N_TILE], F32, name="front")
                     for g in range(PASSES):
                         nc.tensor.matmul_mx(
@@ -166,88 +214,77 @@ def tile_sam_pb_kernel(tc, logits, x, w3c_words, w3c_scales, b3c, out):
                             start=(g == 0),
                             stop=(g == PASSES - 1),
                         )
-                    nc.scalar.copy(
+                    nc.vector.tensor_copy(
                         out=x3T[:, pair, :, heads_per_tile * ot : heads_per_tile * (ot + 1)],
                         in_=acc[:].rearrange("p (h s) -> p s h", s=SP),
                     )
-
-        x3 = keep.tile([P, HEAD_GROUPS, B, SIDE, PADDED, SP], F32)
-        for pair in range(PAIRS):
-            for hg in range(HEAD_GROUPS):
-                for s0 in range(0, SP, 4):
-                    flipped = front_psum.tile([P, 4, 2, HW], F32, name="front")
-                    for k in range(4):
-                        nc.tensor.transpose(
-                            flipped[:, k].rearrange("p x m -> p (x m)"),
-                            x3T[:, pair, s0 + k, P * hg : P * (hg + 1)],
-                            identity[:],
-                        )
+                if u + 1 < len(units):
                     for xb in range(2):
-                        nc.scalar.copy(
-                            out=x3[:, hg, 2 * pair + xb, :, PAD : PAD + SIDE, s0 : s0 + 4],
-                            in_=flipped[:, :, xb, :].rearrange("p s (i j) -> p i j s", i=SIDE),
-                        )
-        image_rows = x3[:].rearrange("p g b i c s -> p (g b i) c s")
-        for c in [c for c in range(PADDED) if mirror(c - PAD) != c - PAD]:
-            nc.scalar.copy(out=image_rows[:, :, c, :], in_=image_rows[:, :, mirror(c - PAD) + PAD, :])
+                        maximum(u + 1, xb)
+
+        late = ctx.enter_context(tc.tile_pool(name="late", bufs=2))
+        inv_ready = fold(ready[0], ready[1])
+        x3_ready = heads_to_partitions(0)
 
         for u, (hg, pair) in enumerate(units):
-            e, inv_total = ready
+            e, inv_total, x3 = ready[0], inv_ready, x3_ready
             if u + 1 < len(units):
-                ready = softmax_numerators(units[u + 1][0], units[u + 1][1])
-            sums = [
-                sum_psum.tile([P, BANK_ROWS, P], F32, name="sums%d" % half) for half in range(SIDE // BANK_ROWS)
-            ]
+                x3_ready = heads_to_partitions(u + 1)
+                ready = numerators(u + 1)
+            by_pos = e[:].rearrange("p (i j) x l -> p i j x l", i=SIDE)
+            sums = [sum_psum.tile([P, BANK_ROWS, P], F32, name="sums%d" % bank) for bank in range(BANKS)]
+            rows_of = [(l, i) for l in range(KK) for i in range(inside(l // WIN)[0], inside(l // WIN)[1])]
+            first = [min([k for k, (l, i) in enumerate(rows_of) if i // BANK_ROWS == bank]) for bank in range(BANKS)]
+            last = [max([k for k, (l, i) in enumerate(rows_of) if i // BANK_ROWS == bank]) for bank in range(BANKS)]
+            k = 0
             for l in range(KK):
                 dy, dx = divmod(l, WIN)
-                i0, i1 = max(0, PAD - dy), min(SIDE, SIDE + PAD - dy)
-                prod = prod_pool.tile([P, SIDE, 2, SIDE, SP], F32, name="prod")
-                nc.vector.tensor_tensor(
-                    out=prod[:, i0:i1].rearrange("p i x j s -> p x i j s"),
-                    in0=x3[:, hg, 2 * pair : 2 * pair + 2, i0 + dy - PAD : i1 + dy - PAD, dx : dx + SIDE, :],
-                    in1=e[:, :, SIDE * i0 : SIDE * i1, l]
-                    .rearrange("p x (i j) -> p x i j", j=SIDE)
-                    .unsqueeze(4)
-                    .to_broadcast([P, 2, i1 - i0, SIDE, SP]),
-                    op=ALU.mult,
-                )
+                i0, i1 = inside(dy)
+                j0, j1 = inside(dx)
+                prod = prod_tiles[(dx, dy % PROD_BUFS)]
+                for h in range(SP // SH):
+                    nc.vector.tensor_tensor(
+                        out=prod[:, i0:i1, j0:j1, :, SH * h : SH * (h + 1)],
+                        in0=x3[h][:, i0 + dy - PAD : i1 + dy - PAD, j0 + dx - PAD : j1 + dx - PAD, :, :],
+                        in1=by_pos[:, i0:i1, j0:j1, :, l].unsqueeze(4).to_broadcast([P, i1 - i0, j1 - j0, 2, SH]),
+                        op=ALU.mult,
+                    )
                 for i in range(i0, i1):
-                    half = i // BANK_ROWS
-                    first_in_bank = max(i0, BANK_ROWS * half)
-                    last_in_bank = min(i1, BANK_ROWS * (half + 1)) - 1
+                    bank = i // BANK_ROWS
                     nc.tensor.matmul(
-                        out=sums[half][:, i % BANK_ROWS, :],
-                        lhsT=prod[:, i].rearrange("p x j s -> p (x j s)"),
+                        out=sums[bank][:, i % BANK_ROWS, :],
+                        lhsT=prod[:, i].rearrange("p j x s -> p (j x s)"),
                         rhs=identity[:],
                         is_transpose=True,
-                        start=(l == 0 and i == first_in_bank),
-                        stop=(l == KK - 1 and i == last_in_bank),
+                        start=(k == first[bank]),
+                        stop=(k == last[bank]),
                     )
+                    k += 1
+            if u + 1 < len(units):
+                inv_ready = fold(ready[0], ready[1])
 
-            y = stream.tile([P, 2, SP, HW], F32, name="y")
-            for half in range(SIDE // BANK_ROWS):
-                sums_sb = stream.tile([P, BANK_ROWS, P], F32, name="sums_sb")
-                nc.scalar.copy(out=sums_sb[:], in_=sums[half][:])
-                back = back_psum.tile([P, BANK_ROWS, 2, SIDE, SP], F32)
-                for k in range(BANK_ROWS):
-                    nc.tensor.transpose(back[:, k].rearrange("p x j s -> p (x j s)"), sums_sb[:, k, :], identity[:])
-                positions = slice(SIDE * BANK_ROWS * half, SIDE * BANK_ROWS * (half + 1))
+            y = late.tile([P, 2, SP, HW], F32, name="y")
+            for bank in range(BANKS):
+                sums_sb = late.tile([P, BANK_ROWS, P], F32, name="sums_sb")
+                nc.scalar.copy(out=sums_sb[:], in_=sums[bank][:])
+                back = front_psum.tile([P, BANK_ROWS, SIDE, 2, SP], F32, name="front")
+                for r in range(BANK_ROWS):
+                    nc.tensor.transpose(back[:, r].rearrange("p j x s -> p (j x s)"), sums_sb[:, r, :], identity[:])
+                positions = slice(SIDE * BANK_ROWS * bank, SIDE * BANK_ROWS * (bank + 1))
                 for xb in range(2):
                     nc.vector.tensor_tensor(
                         out=y[:, xb, :, positions].rearrange("p s (i j) -> p s i j", j=SIDE),
-                        in0=back[:, :, xb].rearrange("p i j s -> p s i j"),
-                        in1=inv_total[:, xb, positions]
+                        in0=back[:, :, :, xb, :].rearrange("p i j s -> p s i j"),
+                        in1=inv_total[:, positions, xb]
                         .rearrange("p (i j) -> p i j", j=SIDE)
                         .unsqueeze(1)
                         .to_broadcast([P, SP, BANK_ROWS, SIDE]),
                         op=ALU.mult,
                     )
-            nc.vector.tensor_tensor(
-                out=y[:],
-                in0=y[:],
-                in1=bias[:, hg, :].unsqueeze(1).unsqueeze(3).to_broadcast([P, 2, SP, HW]),
-                op=ALU.add,
-            )
+            for s in range(SP):
+                nc.scalar.activation(
+                    out=y[:, :, s, :], in_=y[:, :, s, :], func=ACT.Identity, bias=bias[:, hg, s : s + 1], scale=1.0
+                )
             for xb in range(2):
                 nc.sync.dma_start(
                     out=out[2 * pair + xb, SP * P * hg : SP * P * (hg + 1)].rearrange("(r s) i j -> r (s i j)", s=SP),

@@ -29,6 +29,8 @@ BANKS = SIDE // BANK_ROWS
 PITCH = 52
 SH = SP // 2
 PROD_BUFS = 2
+GP_EVERY = 3
+FINISH_AFTER = 6
 
 FLOPS = 2 * B * HW * CIN * COUT + 2 * B * COUT * HW * KK
 
@@ -49,6 +51,10 @@ def outside_offsets():
             if mirror(u) != u:
                 found.append((i, dy, mirror(u) - i + PAD))
     return found
+
+
+def on_gpsimd(l):
+    return l // WIN <= PAD and l % WIN in (PAD, PAD + 1)
 
 
 def inside(d):
@@ -119,7 +125,7 @@ def tile_sam_pb_kernel(tc, logits, x, w3c_words, w3c_scales, b3c, out):
                     )
             return e, total
 
-        def fold(e, total):
+        def fold(e):
             view = e[:, :, :, 0:KK].rearrange("p (i j) x (dy dx) -> p i j x dy dx", i=SIDE, dy=WIN)
             for i, src, dst in folds:
                 nc.gpsimd.tensor_tensor(
@@ -129,6 +135,8 @@ def tile_sam_pb_kernel(tc, logits, x, w3c_words, w3c_scales, b3c, out):
                 nc.gpsimd.tensor_tensor(
                     out=view[:, :, j, :, :, dst], in0=view[:, :, j, :, :, dst], in1=view[:, :, j, :, :, src], op=ALU.add
                 )
+
+        def invert(total):
             inv_total = stream.tile([P, HW, 2], F32, name="inv_total")
             nc.vector.reciprocal(out=inv_total[:], in_=total[:])
             return inv_total
@@ -144,7 +152,10 @@ def tile_sam_pb_kernel(tc, logits, x, w3c_words, w3c_scales, b3c, out):
                     x3T[:, pair, s, P * hg : P * (hg + 1)],
                     identity[:],
                 )
-            return banks
+            x3_sb = late.tile([P, SIDE, SIDE, 2, SP], F32, name="x3_sb")
+            for h in range(SP // SH):
+                nc.scalar.copy(out=x3_sb[:, :, :, :, SH * h : SH * (h + 1)], in_=banks[h][:])
+            return banks, x3_sb
 
         bias_bf = keep.tile([P, HEAD_GROUPS, SP], BF16)
         bias = keep.tile([P, HEAD_GROUPS, SP], F32)
@@ -223,58 +234,31 @@ def tile_sam_pb_kernel(tc, logits, x, w3c_words, w3c_scales, b3c, out):
                         maximum(u + 1, xb)
 
         late = ctx.enter_context(tc.tile_pool(name="late", bufs=2))
-        inv_ready = fold(ready[0], ready[1])
+        fold(ready[0])
+        inv_ready = invert(ready[1])
         x3_ready = heads_to_partitions(0)
 
-        for u, (hg, pair) in enumerate(units):
-            e, inv_total, x3 = ready[0], inv_ready, x3_ready
-            if u + 1 < len(units):
-                x3_ready = heads_to_partitions(u + 1)
-                ready = numerators(u + 1)
-            by_pos = e[:].rearrange("p (i j) x l -> p i j x l", i=SIDE)
-            sums = [sum_psum.tile([P, BANK_ROWS, P], F32, name="sums%d" % bank) for bank in range(BANKS)]
-            rows_of = [(l, i) for l in range(KK) for i in range(inside(l // WIN)[0], inside(l // WIN)[1])]
-            first = [min([k for k, (l, i) in enumerate(rows_of) if i // BANK_ROWS == bank]) for bank in range(BANKS)]
-            last = [max([k for k, (l, i) in enumerate(rows_of) if i // BANK_ROWS == bank]) for bank in range(BANKS)]
-            k = 0
-            for l in range(KK):
-                dy, dx = divmod(l, WIN)
-                i0, i1 = inside(dy)
-                j0, j1 = inside(dx)
-                prod = prod_tiles[(dx, dy % PROD_BUFS)]
-                for h in range(SP // SH):
-                    nc.vector.tensor_tensor(
-                        out=prod[:, i0:i1, j0:j1, :, SH * h : SH * (h + 1)],
-                        in0=x3[h][:, i0 + dy - PAD : i1 + dy - PAD, j0 + dx - PAD : j1 + dx - PAD, :, :],
-                        in1=by_pos[:, i0:i1, j0:j1, :, l].unsqueeze(4).to_broadcast([P, i1 - i0, j1 - j0, 2, SH]),
-                        op=ALU.mult,
-                    )
-                for i in range(i0, i1):
-                    bank = i // BANK_ROWS
-                    nc.tensor.matmul(
-                        out=sums[bank][:, i % BANK_ROWS, :],
-                        lhsT=prod[:, i].rearrange("p j x s -> p (j x s)"),
-                        rhs=identity[:],
-                        is_transpose=True,
-                        start=(k == first[bank]),
-                        stop=(k == last[bank]),
-                    )
-                    k += 1
-            if u + 1 < len(units):
-                inv_ready = fold(ready[0], ready[1])
+        vector_list = [l for l in range(KK) if not on_gpsimd(l)]
+        gpsimd_list = [l for l in range(KK) if on_gpsimd(l)]
+        order = []
+        for k, l in enumerate(vector_list):
+            order.append(l)
+            if k % GP_EVERY == GP_EVERY - 1 and k // GP_EVERY < len(gpsimd_list):
+                order.append(gpsimd_list[k // GP_EVERY])
+        assert len(order) == KK
+        rows_of = [(l, i) for l in order for i in range(inside(l // WIN)[0], inside(l // WIN)[1])]
+        first = [min([k for k, (l, i) in enumerate(rows_of) if i // BANK_ROWS == bank]) for bank in range(BANKS)]
+        last = [max([k for k, (l, i) in enumerate(rows_of) if i // BANK_ROWS == bank]) for bank in range(BANKS)]
 
+        def finish(u, backs, inv_total):
+            hg, pair = units[u]
             y = late.tile([P, 2, SP, HW], F32, name="y")
             for bank in range(BANKS):
-                sums_sb = late.tile([P, BANK_ROWS, P], F32, name="sums_sb")
-                nc.scalar.copy(out=sums_sb[:], in_=sums[bank][:])
-                back = front_psum.tile([P, BANK_ROWS, SIDE, 2, SP], F32, name="front")
-                for r in range(BANK_ROWS):
-                    nc.tensor.transpose(back[:, r].rearrange("p j x s -> p (j x s)"), sums_sb[:, r, :], identity[:])
                 positions = slice(SIDE * BANK_ROWS * bank, SIDE * BANK_ROWS * (bank + 1))
                 for xb in range(2):
                     nc.vector.tensor_tensor(
                         out=y[:, xb, :, positions].rearrange("p s (i j) -> p s i j", j=SIDE),
-                        in0=back[:, :, :, xb, :].rearrange("p i j s -> p s i j"),
+                        in0=backs[bank][:, :, :, xb, :].rearrange("p i j s -> p s i j"),
                         in1=inv_total[:, positions, xb]
                         .rearrange("p (i j) -> p i j", j=SIDE)
                         .unsqueeze(1)
@@ -290,3 +274,62 @@ def tile_sam_pb_kernel(tc, logits, x, w3c_words, w3c_scales, b3c, out):
                     out=out[2 * pair + xb, SP * P * hg : SP * P * (hg + 1)].rearrange("(r s) i j -> r (s i j)", s=SP),
                     in_=y[:, xb].rearrange("p s n -> p (s n)"),
                 )
+
+        waiting = None
+        for u, (hg, pair) in enumerate(units):
+            e, inv_total = ready[0], inv_ready
+            x3, x3_sb = x3_ready
+            if u + 1 < len(units):
+                x3_ready = heads_to_partitions(u + 1)
+                ready = numerators(u + 1)
+            by_pos = e[:].rearrange("p (i j) x l -> p i j x l", i=SIDE)
+            sums = [sum_psum.tile([P, BANK_ROWS, P], F32, name="sums%d" % bank) for bank in range(BANKS)]
+            k = 0
+            for place, l in enumerate(order):
+                dy, dx = divmod(l, WIN)
+                i0, i1 = inside(dy)
+                j0, j1 = inside(dx)
+                prod = prod_tiles[(dx, dy % PROD_BUFS)]
+                if on_gpsimd(l):
+                    nc.gpsimd.tensor_tensor(
+                        out=prod[:, i0:i1, j0:j1, :, :],
+                        in0=x3_sb[:, i0 + dy - PAD : i1 + dy - PAD, j0 + dx - PAD : j1 + dx - PAD, :, :],
+                        in1=by_pos[:, i0:i1, j0:j1, :, l].unsqueeze(4).to_broadcast([P, i1 - i0, j1 - j0, 2, SP]),
+                        op=ALU.mult,
+                    )
+                    if l == gpsimd_list[-1] and u + 1 < len(units):
+                        fold(ready[0])
+                else:
+                    for h in range(SP // SH):
+                        nc.vector.tensor_tensor(
+                            out=prod[:, i0:i1, j0:j1, :, SH * h : SH * (h + 1)],
+                            in0=x3[h][:, i0 + dy - PAD : i1 + dy - PAD, j0 + dx - PAD : j1 + dx - PAD, :, :],
+                            in1=by_pos[:, i0:i1, j0:j1, :, l].unsqueeze(4).to_broadcast([P, i1 - i0, j1 - j0, 2, SH]),
+                            op=ALU.mult,
+                        )
+                for i in range(i0, i1):
+                    bank = i // BANK_ROWS
+                    nc.tensor.matmul(
+                        out=sums[bank][:, i % BANK_ROWS, :],
+                        lhsT=prod[:, i].rearrange("p j x s -> p (j x s)"),
+                        rhs=identity[:],
+                        is_transpose=True,
+                        start=(k == first[bank]),
+                        stop=(k == last[bank]),
+                    )
+                    k += 1
+                if place == FINISH_AFTER and waiting is not None:
+                    finish(waiting[0], waiting[1], waiting[2])
+            if u + 1 < len(units):
+                inv_ready = invert(ready[1])
+
+            backs = []
+            for bank in range(BANKS):
+                sums_sb = late.tile([P, BANK_ROWS, P], F32, name="sums_sb")
+                nc.scalar.copy(out=sums_sb[:], in_=sums[bank][:])
+                back = front_psum.tile([P, BANK_ROWS, SIDE, 2, SP], F32, name="front")
+                for r in range(BANK_ROWS):
+                    nc.tensor.transpose(back[:, r].rearrange("p j x s -> p (j x s)"), sums_sb[:, r, :], identity[:])
+                backs.append(back)
+            waiting = (u, backs, inv_total)
+        finish(waiting[0], waiting[1], waiting[2])

@@ -31,6 +31,8 @@ SH = SP // 2
 PROD_BUFS = 2
 GP_EVERY = 3
 FINISH_AFTER = 6
+PROJECT_AFTER = (14, 30)
+X3_AFTER = 40
 
 FLOPS = 2 * B * HW * CIN * COUT + 2 * B * COUT * HW * KK
 
@@ -141,15 +143,38 @@ def tile_sam_pb_kernel(tc, logits, x, w3c_words, w3c_scales, b3c, out):
             nc.vector.reciprocal(out=inv_total[:], in_=total[:])
             return inv_total
 
-        x3T = keep.tile([P, PAIRS, SP, COUT // SP], F32)
+        x_codes = keep.tile([P, PASSES, B * HW], U32, align_bytes=64)
+        x_scales = keep.tile([P, PASSES, B * HW], U8, align_bytes=64)
+        w_scales = keep.tile([P, PASSES, COUT], U8, align_bytes=64)
+        w_words = keep.tile([P, PASSES, 2 * COUT], U8, align_bytes=64)
+        heads_per_tile = N_TILE // SP
 
-        def heads_to_partitions(u):
+        def project(u, x3T, part):
             hg, pair = units[u]
+            cols = slice(P * pair, P * (pair + 1))
+            ot = 2 * hg + part
+            acc = front_psum.tile([P, N_TILE], F32, name="front")
+            for g in range(PASSES):
+                nc.tensor.matmul_mx(
+                    out=acc[:],
+                    lhsT=x_codes[:, g, cols].bitcast(FP8X4),
+                    lhsT_scale=x_scales[:, g, cols],
+                    rhs=w_words[:, g, 2 * N_TILE * ot : 2 * N_TILE * (ot + 1)].bitcast(FP4X4),
+                    rhs_scale=w_scales[:, g, N_TILE * ot : N_TILE * (ot + 1)],
+                    start=(g == 0),
+                    stop=(g == PASSES - 1),
+                )
+            nc.scalar.copy(
+                out=x3T[:, :, heads_per_tile * part : heads_per_tile * (part + 1)],
+                in_=acc[:].rearrange("p (h s) -> p s h", s=SP),
+            )
+
+        def heads_to_partitions(x3T):
             banks = [x3_psum.tile([P, SIDE, SIDE, 2, SH], F32, name="x3_%d" % h) for h in range(SP // SH)]
             for s in range(SP):
                 nc.tensor.transpose(
                     banks[s // SH][:].rearrange("p i j x s -> p (i j x) s")[:, :, s % SH],
-                    x3T[:, pair, s, P * hg : P * (hg + 1)],
+                    x3T[:, s, :],
                     identity[:],
                 )
             x3_sb = late.tile([P, SIDE, SIDE, 2, SP], F32, name="x3_sb")
@@ -161,7 +186,6 @@ def tile_sam_pb_kernel(tc, logits, x, w3c_words, w3c_scales, b3c, out):
         bias = keep.tile([P, HEAD_GROUPS, SP], F32)
 
         with tc.tile_pool(name="front", bufs=1) as front:
-            w_scales = front.tile([P, PASSES, COUT], U8, align_bytes=64)
             nc.vector.memset(w_scales[:].rearrange("p g n -> p (g n)").bitcast(I32), 0)
 
             load_logits(0, 0)
@@ -176,7 +200,6 @@ def tile_sam_pb_kernel(tc, logits, x, w3c_words, w3c_scales, b3c, out):
                         out=w_scales[32 * half + r : P : 64, :, :].bitcast(I32),
                         in_=w3c_scales[:, 4 * half + r : 16 : 8, :].rearrange("g q n -> q g n").bitcast(I32),
                     )
-            w_words = front.tile([P, PASSES, 2 * COUT], U8, align_bytes=64)
             for hg in range(HEAD_GROUPS):
                 for g in range(PASSES):
                     nc.sync.dma_start(
@@ -194,8 +217,6 @@ def tile_sam_pb_kernel(tc, logits, x, w3c_words, w3c_scales, b3c, out):
             ready = numerators(0)
 
             x_grouped = front.tile([P, PASSES, B * HW, PACK], BF16, align_bytes=64)
-            x_codes = front.tile([P, PASSES, B * HW], U32, align_bytes=64)
-            x_scales = front.tile([P, PASSES, B * HW], U8, align_bytes=64)
             for g in range(PASSES):
                 for pair in range(PAIRS):
                     nc.vector.tensor_copy(
@@ -210,33 +231,17 @@ def tile_sam_pb_kernel(tc, logits, x, w3c_words, w3c_scales, b3c, out):
                 )
             nc.vector.tensor_copy(out=bias[:], in_=bias_bf[:])
 
-            heads_per_tile = N_TILE // SP
-            for u, (hg, pair) in enumerate(units):
-                cols = slice(P * pair, P * (pair + 1))
-                for ot in range(2 * hg, 2 * hg + 2):
-                    acc = front_psum.tile([P, N_TILE], F32, name="front")
-                    for g in range(PASSES):
-                        nc.tensor.matmul_mx(
-                            out=acc[:],
-                            lhsT=x_codes[:, g, cols].bitcast(FP8X4),
-                            lhsT_scale=x_scales[:, g, cols],
-                            rhs=w_words[:, g, 2 * N_TILE * ot : 2 * N_TILE * (ot + 1)].bitcast(FP4X4),
-                            rhs_scale=w_scales[:, g, N_TILE * ot : N_TILE * (ot + 1)],
-                            start=(g == 0),
-                            stop=(g == PASSES - 1),
-                        )
-                    nc.vector.tensor_copy(
-                        out=x3T[:, pair, :, heads_per_tile * ot : heads_per_tile * (ot + 1)],
-                        in_=acc[:].rearrange("p (h s) -> p s h", s=SP),
-                    )
-                if u + 1 < len(units):
-                    for xb in range(2):
-                        maximum(u + 1, xb)
+            for u in range(1, len(units)):
+                for xb in range(2):
+                    maximum(u, xb)
 
         late = ctx.enter_context(tc.tile_pool(name="late", bufs=2))
         fold(ready[0])
         inv_ready = invert(ready[1])
-        x3_ready = heads_to_partitions(0)
+        x3T = stream.tile([P, SP, P], F32, name="x3T")
+        project(0, x3T, 0)
+        project(0, x3T, 1)
+        x3_ready = heads_to_partitions(x3T)
 
         vector_list = [l for l in range(KK) if not on_gpsimd(l)]
         gpsimd_list = [l for l in range(KK) if on_gpsimd(l)]
@@ -280,8 +285,8 @@ def tile_sam_pb_kernel(tc, logits, x, w3c_words, w3c_scales, b3c, out):
             e, inv_total = ready[0], inv_ready
             x3, x3_sb = x3_ready
             if u + 1 < len(units):
-                x3_ready = heads_to_partitions(u + 1)
                 ready = numerators(u + 1)
+                x3T = stream.tile([P, SP, P], F32, name="x3T")
             by_pos = e[:].rearrange("p (i j) x l -> p i j x l", i=SIDE)
             sums = [sum_psum.tile([P, BANK_ROWS, P], F32, name="sums%d" % bank) for bank in range(BANKS)]
             k = 0
@@ -320,6 +325,10 @@ def tile_sam_pb_kernel(tc, logits, x, w3c_words, w3c_scales, b3c, out):
                     k += 1
                 if place == FINISH_AFTER and waiting is not None:
                     finish(waiting[0], waiting[1], waiting[2])
+                if u + 1 < len(units) and place in PROJECT_AFTER:
+                    project(u + 1, x3T, PROJECT_AFTER.index(place))
+                if u + 1 < len(units) and place == X3_AFTER:
+                    x3_ready = heads_to_partitions(x3T)
             if u + 1 < len(units):
                 inv_ready = invert(ready[1])
 

@@ -29,10 +29,8 @@ BANKS = SIDE // BANK_ROWS
 PITCH = 52
 SH = SP // 2
 PROD_BUFS = 2
-GP_EVERY = 3
+GP_EVERY = 6
 FINISH_AFTER = 6
-PROJECT_AFTER = (14, 30)
-X3_AFTER = 40
 
 FLOPS = 2 * B * HW * CIN * COUT + 2 * B * COUT * HW * KK
 
@@ -56,17 +54,31 @@ def outside_offsets():
 
 
 def on_gpsimd(l):
-    return l // WIN <= PAD and l % WIN in (PAD, PAD + 1)
+    return l // WIN <= PAD and l % WIN == PAD
 
 
 def inside(d):
     return max(0, PAD - d), min(SIDE, SIDE + PAD - d)
 
 
+def product_tasks(ranges, with_gpsimd):
+    tasks = []
+    for r0, r1 in ranges:
+        mine = [(l, max(r0, inside(l // WIN)[0]), min(r1, inside(l // WIN)[1])) for l in range(KK)]
+        vector_list = [t for t in mine if not (with_gpsimd and on_gpsimd(t[0]))]
+        gpsimd_list = [t for t in mine if with_gpsimd and on_gpsimd(t[0])]
+        for k, t in enumerate(vector_list):
+            tasks.append(t)
+            if k % GP_EVERY == GP_EVERY - 1 and k // GP_EVERY < len(gpsimd_list):
+                tasks.append(gpsimd_list[k // GP_EVERY])
+    return tasks
+
+
 def tile_sam_pb_kernel(tc, logits, x, w3c_words, w3c_scales, b3c, out):
     nc = tc.nc
     folds = outside_offsets()
     units = [(hg, pair) for hg in range(HEAD_GROUPS) for pair in range(PAIRS)]
+    halves = [(0, SIDE // 2), (SIDE // 2, SIDE)]
     with ExitStack() as ctx:
         keep = ctx.enter_context(tc.tile_pool(name="keep", bufs=1))
         stream = ctx.enter_context(tc.tile_pool(name="stream", bufs=2))
@@ -78,8 +90,10 @@ def tile_sam_pb_kernel(tc, logits, x, w3c_words, w3c_scales, b3c, out):
         make_identity(nc, identity[:])
 
         prod_tiles = {}
+        uses = {}
         for dx in range(WIN):
             j0, j1 = inside(dx)
+            uses[dx] = 0
             for k in range(PROD_BUFS):
                 t = keep.tile([P, SIDE, SIDE, 2, SP], F32, name="prod_%d_%d" % (dx, k))
                 if j0 > 0:
@@ -95,27 +109,30 @@ def tile_sam_pb_kernel(tc, logits, x, w3c_words, w3c_scales, b3c, out):
             hg, pair = units[u]
             nc.sync.dma_start(out=lg[u][:, xb], in_=logits[2 * pair + xb, P * hg : P * (hg + 1)])
 
-        def maximum(u, xb):
-            top = stream.tile([P, KK // 2, HW], BF16, name="top")
-            nc.vector.tensor_tensor(
-                out=top[:], in0=lg[u][:, xb, 0 : KK // 2, :], in1=lg[u][:, xb, KK // 2 + 1 : KK, :], op=ALU.max
-            )
-            rows = KK // 2
-            while rows > 1:
-                half = rows // 2
+        def maximum(u, i0, i1):
+            n0, n1 = SIDE * i0, SIDE * i1
+            for xb in range(2):
+                top = stream.tile([P, KK // 2, n1 - n0], BF16, name="top")
                 nc.vector.tensor_tensor(
-                    out=top[:, 0:half, :], in0=top[:, 0:half, :], in1=top[:, rows - half : rows, :], op=ALU.max
+                    out=top[:],
+                    in0=lg[u][:, xb, 0 : KK // 2, n0:n1],
+                    in1=lg[u][:, xb, KK // 2 + 1 : KK, n0:n1],
+                    op=ALU.max,
                 )
-                rows = rows - half
-            nc.vector.tensor_tensor(
-                out=top[:, 0:1, :], in0=top[:, 0:1, :], in1=lg[u][:, xb, KK // 2 : KK // 2 + 1, :], op=ALU.max
-            )
-            nc.vector.tensor_scalar_mul(out=minus_top[u][:, :, xb], in0=top[:, 0, :], scalar1=-1.0)
+                rows = KK // 2
+                while rows > 1:
+                    half = rows // 2
+                    nc.vector.tensor_tensor(
+                        out=top[:, 0:half, :], in0=top[:, 0:half, :], in1=top[:, rows - half : rows, :], op=ALU.max
+                    )
+                    rows = rows - half
+                nc.vector.tensor_tensor(
+                    out=top[:, 0:1, :], in0=top[:, 0:1, :], in1=lg[u][:, xb, KK // 2 : KK // 2 + 1, n0:n1], op=ALU.max
+                )
+                nc.vector.tensor_scalar_mul(out=minus_top[u][:, n0:n1, xb], in0=top[:, 0, :], scalar1=-1.0)
 
-        def numerators(u):
-            e = stream.tile([P, HW, 2, PITCH], F32, name="e")
-            total = stream.tile([P, HW, 2], F32, name="total")
-            for n in range(HW):
+        def numerators(u, e, total, i0, i1):
+            for n in range(SIDE * i0, SIDE * i1):
                 for xb in range(2):
                     nc.scalar.activation(
                         out=e[:, n, xb, 0:KK],
@@ -125,17 +142,23 @@ def tile_sam_pb_kernel(tc, logits, x, w3c_words, w3c_scales, b3c, out):
                         scale=1.0,
                         accum_out=total[:, n, xb : xb + 1],
                     )
-            return e, total
 
-        def fold(e):
+        def fold(e, i0, i1, engine):
             view = e[:, :, :, 0:KK].rearrange("p (i j) x (dy dx) -> p i j x dy dx", i=SIDE, dy=WIN)
             for i, src, dst in folds:
-                nc.gpsimd.tensor_tensor(
-                    out=view[:, i, :, :, dst, :], in0=view[:, i, :, :, dst, :], in1=view[:, i, :, :, src, :], op=ALU.add
-                )
+                if i0 <= i < i1:
+                    engine.tensor_tensor(
+                        out=view[:, i, :, :, dst, :],
+                        in0=view[:, i, :, :, dst, :],
+                        in1=view[:, i, :, :, src, :],
+                        op=ALU.add,
+                    )
             for j, src, dst in folds:
-                nc.gpsimd.tensor_tensor(
-                    out=view[:, :, j, :, :, dst], in0=view[:, :, j, :, :, dst], in1=view[:, :, j, :, :, src], op=ALU.add
+                engine.tensor_tensor(
+                    out=view[:, i0:i1, j, :, :, dst],
+                    in0=view[:, i0:i1, j, :, :, dst],
+                    in1=view[:, i0:i1, j, :, :, src],
+                    op=ALU.add,
                 )
 
         def invert(total):
@@ -164,12 +187,13 @@ def tile_sam_pb_kernel(tc, logits, x, w3c_words, w3c_scales, b3c, out):
                     start=(g == 0),
                     stop=(g == PASSES - 1),
                 )
-            nc.scalar.copy(
-                out=x3T[:, :, heads_per_tile * part : heads_per_tile * (part + 1)],
-                in_=acc[:].rearrange("p (h s) -> p s h", s=SP),
-            )
+            target = x3T[:, :, heads_per_tile * part : heads_per_tile * (part + 1)]
+            if u == 0:
+                nc.vector.tensor_copy(out=target, in_=acc[:].rearrange("p (h s) -> p s h", s=SP))
+            else:
+                nc.scalar.copy(out=target, in_=acc[:].rearrange("p (h s) -> p s h", s=SP))
 
-        def heads_to_partitions(x3T):
+        def heads_to_partitions(x3T, for_gpsimd):
             banks = [x3_psum.tile([P, SIDE, SIDE, 2, SH], F32, name="x3_%d" % h) for h in range(SP // SH)]
             for s in range(SP):
                 nc.tensor.transpose(
@@ -177,22 +201,27 @@ def tile_sam_pb_kernel(tc, logits, x, w3c_words, w3c_scales, b3c, out):
                     x3T[:, s, :],
                     identity[:],
                 )
-            x3_sb = late.tile([P, SIDE, SIDE, 2, SP], F32, name="x3_sb")
-            for h in range(SP // SH):
-                nc.scalar.copy(out=x3_sb[:, :, :, :, SH * h : SH * (h + 1)], in_=banks[h][:])
+            x3_sb = None
+            if for_gpsimd:
+                x3_sb = late.tile([P, SIDE, SIDE, 2, SP], F32, name="x3_sb")
+                for h in range(SP // SH):
+                    nc.scalar.copy(out=x3_sb[:, :, :, :, SH * h : SH * (h + 1)], in_=banks[h][:])
             return banks, x3_sb
 
         bias_bf = keep.tile([P, HEAD_GROUPS, SP], BF16)
         bias = keep.tile([P, HEAD_GROUPS, SP], F32)
+        e_ready = stream.tile([P, HW, 2, PITCH], F32, name="e")
+        total_ready = stream.tile([P, HW, 2], F32, name="total")
 
         with tc.tile_pool(name="front", bufs=1) as front:
             nc.vector.memset(w_scales[:].rearrange("p g n -> p (g n)").bitcast(I32), 0)
 
-            load_logits(0, 0)
             x_raw = front.tile([P, B, PASSES, PACK, HW], BF16)
-            nc.sync.dma_start(
+            nc.scalar.dma_start(
                 out=x_raw[:], in_=x.rearrange("b (g p t) i j -> p b g t (i j)", g=PASSES, p=P, t=PACK)
             )
+            nc.scalar.dma_start(out=bias_bf[:], in_=b3c.rearrange("(g r s) -> r g s", g=HEAD_GROUPS, r=P))
+            load_logits(0, 0)
             load_logits(0, 1)
             for half in range(2):
                 for r in range(4):
@@ -210,11 +239,10 @@ def tile_sam_pb_kernel(tc, logits, x, w3c_words, w3c_scales, b3c, out):
                     load_logits(1 + hg, xb)
             for xb in range(2):
                 load_logits(3, xb)
-            nc.scalar.dma_start(out=bias_bf[:], in_=b3c.rearrange("(g r s) -> r g s", g=HEAD_GROUPS, r=P))
 
-            maximum(0, 0)
-            maximum(0, 1)
-            ready = numerators(0)
+            for i0, i1 in halves:
+                maximum(0, i0, i1)
+                numerators(0, e_ready, total_ready, i0, i1)
 
             x_grouped = front.tile([P, PASSES, B * HW, PACK], BF16, align_bytes=64)
             for g in range(PASSES):
@@ -230,30 +258,15 @@ def tile_sam_pb_kernel(tc, logits, x, w3c_words, w3c_scales, b3c, out):
                     in_=x_grouped[:, g].rearrange("p c t -> p (c t)"),
                 )
             nc.vector.tensor_copy(out=bias[:], in_=bias_bf[:])
-
-            for u in range(1, len(units)):
-                for xb in range(2):
-                    maximum(u, xb)
+            maximum(1, 0, SIDE)
 
         late = ctx.enter_context(tc.tile_pool(name="late", bufs=2))
-        fold(ready[0])
-        inv_ready = invert(ready[1])
         x3T = stream.tile([P, SP, P], F32, name="x3T")
         project(0, x3T, 0)
         project(0, x3T, 1)
-        x3_ready = heads_to_partitions(x3T)
-
-        vector_list = [l for l in range(KK) if not on_gpsimd(l)]
-        gpsimd_list = [l for l in range(KK) if on_gpsimd(l)]
-        order = []
-        for k, l in enumerate(vector_list):
-            order.append(l)
-            if k % GP_EVERY == GP_EVERY - 1 and k // GP_EVERY < len(gpsimd_list):
-                order.append(gpsimd_list[k // GP_EVERY])
-        assert len(order) == KK
-        rows_of = [(l, i) for l in order for i in range(inside(l // WIN)[0], inside(l // WIN)[1])]
-        first = [min([k for k, (l, i) in enumerate(rows_of) if i // BANK_ROWS == bank]) for bank in range(BANKS)]
-        last = [max([k for k, (l, i) in enumerate(rows_of) if i // BANK_ROWS == bank]) for bank in range(BANKS)]
+        x3_ready = heads_to_partitions(x3T, False)
+        fold(e_ready, halves[0][0], halves[0][1], nc.vector)
+        fold(e_ready, halves[1][0], halves[1][1], nc.gpsimd)
 
         def finish(u, backs, inv_total):
             hg, pair = units[u]
@@ -282,28 +295,36 @@ def tile_sam_pb_kernel(tc, logits, x, w3c_words, w3c_scales, b3c, out):
 
         waiting = None
         for u, (hg, pair) in enumerate(units):
-            e, inv_total = ready[0], inv_ready
+            e, total = e_ready, total_ready
             x3, x3_sb = x3_ready
-            if u + 1 < len(units):
-                ready = numerators(u + 1)
+            more = u + 1 < len(units)
+            tasks = product_tasks(halves if u == 0 else [(0, SIDE)], u > 0)
+            rows_of = [(place, i) for place, t in enumerate(tasks) for i in range(t[1], t[2])]
+            first = [min([k for k, (place, i) in enumerate(rows_of) if i // BANK_ROWS == bank]) for bank in range(BANKS)]
+            last = [max([k for k, (place, i) in enumerate(rows_of) if i // BANK_ROWS == bank]) for bank in range(BANKS)]
+            fold_after = max([0] + [place for place, t in enumerate(tasks) if u > 0 and on_gpsimd(t[0])])
+            if more:
+                if u > 0:
+                    maximum(u + 1, 0, SIDE)
+                e_ready = stream.tile([P, HW, 2, PITCH], F32, name="e")
+                total_ready = stream.tile([P, HW, 2], F32, name="total")
+                numerators(u + 1, e_ready, total_ready, 0, SIDE)
                 x3T = stream.tile([P, SP, P], F32, name="x3T")
             by_pos = e[:].rearrange("p (i j) x l -> p i j x l", i=SIDE)
             sums = [sum_psum.tile([P, BANK_ROWS, P], F32, name="sums%d" % bank) for bank in range(BANKS)]
             k = 0
-            for place, l in enumerate(order):
+            for place, (l, i0, i1) in enumerate(tasks):
                 dy, dx = divmod(l, WIN)
-                i0, i1 = inside(dy)
                 j0, j1 = inside(dx)
-                prod = prod_tiles[(dx, dy % PROD_BUFS)]
-                if on_gpsimd(l):
+                prod = prod_tiles[(dx, uses[dx] % PROD_BUFS)]
+                uses[dx] = uses[dx] + 1
+                if u > 0 and on_gpsimd(l):
                     nc.gpsimd.tensor_tensor(
                         out=prod[:, i0:i1, j0:j1, :, :],
                         in0=x3_sb[:, i0 + dy - PAD : i1 + dy - PAD, j0 + dx - PAD : j1 + dx - PAD, :, :],
                         in1=by_pos[:, i0:i1, j0:j1, :, l].unsqueeze(4).to_broadcast([P, i1 - i0, j1 - j0, 2, SP]),
                         op=ALU.mult,
                     )
-                    if l == gpsimd_list[-1] and u + 1 < len(units):
-                        fold(ready[0])
                 else:
                     for h in range(SP // SH):
                         nc.vector.tensor_tensor(
@@ -325,12 +346,16 @@ def tile_sam_pb_kernel(tc, logits, x, w3c_words, w3c_scales, b3c, out):
                     k += 1
                 if place == FINISH_AFTER and waiting is not None:
                     finish(waiting[0], waiting[1], waiting[2])
-                if u + 1 < len(units) and place in PROJECT_AFTER:
-                    project(u + 1, x3T, PROJECT_AFTER.index(place))
-                if u + 1 < len(units) and place == X3_AFTER:
-                    x3_ready = heads_to_partitions(x3T)
-            if u + 1 < len(units):
-                inv_ready = invert(ready[1])
+                if more and place == fold_after:
+                    for r0, r1 in halves:
+                        fold(e_ready, r0, r1, nc.gpsimd)
+                if more and place == (3 * len(tasks)) // 10:
+                    project(u + 1, x3T, 0)
+                if more and place == (6 * len(tasks)) // 10:
+                    project(u + 1, x3T, 1)
+                if more and place == (8 * len(tasks)) // 10:
+                    x3_ready = heads_to_partitions(x3T, True)
+            inv_total = invert(total)
 
             backs = []
             for bank in range(BANKS):

@@ -88,6 +88,9 @@ def tile_sam_pb_kernel(tc, logits, x, w3c_words, w3c_scales, b3c, out):
 
         identity = keep.tile([P, P], F32)
         make_identity(nc, identity[:])
+        warm = keep.tile([P, 1], F32)
+        nc.vector.memset(warm[:], 0.0)
+        nc.scalar.activation(out=warm[:], in_=warm[:], func=ACT.Exp)
 
         prod_tiles = {}
         uses = {}
@@ -131,6 +134,28 @@ def tile_sam_pb_kernel(tc, logits, x, w3c_words, w3c_scales, b3c, out):
                 )
                 nc.vector.tensor_scalar_mul(out=minus_top[u][:, n0:n1, xb], in0=top[:, 0, :], scalar1=-1.0)
 
+        def maximum_of_pair(u):
+            top = stream.tile([P, 2, KK // 2, HW], BF16, name="top_pair", bufs=1)
+            nc.vector.tensor_tensor(
+                out=top[:], in0=lg[u][:, :, 0 : KK // 2, :], in1=lg[u][:, :, KK // 2 + 1 : KK, :], op=ALU.max
+            )
+            rows = KK // 2
+            while rows > 1:
+                half = rows // 2
+                nc.vector.tensor_tensor(
+                    out=top[:, :, 0:half, :],
+                    in0=top[:, :, 0:half, :],
+                    in1=top[:, :, rows - half : rows, :],
+                    op=ALU.max,
+                )
+                rows = rows - half
+            nc.vector.tensor_tensor(
+                out=top[:, :, 0:1, :], in0=top[:, :, 0:1, :], in1=lg[u][:, :, KK // 2 : KK // 2 + 1, :], op=ALU.max
+            )
+            nc.vector.tensor_scalar_mul(
+                out=minus_top[u][:].rearrange("p n x -> p x n"), in0=top[:, :, 0, :], scalar1=-1.0
+            )
+
         def numerators(u, e, total, i0, i1):
             for n in range(SIDE * i0, SIDE * i1):
                 for xb in range(2):
@@ -143,10 +168,11 @@ def tile_sam_pb_kernel(tc, logits, x, w3c_words, w3c_scales, b3c, out):
                         accum_out=total[:, n, xb : xb + 1],
                     )
 
-        def fold(e, i0, i1, engine):
+        def fold(e, i0, i1, engine, to_dy=None, to_dx=None):
             view = e[:, :, :, 0:KK].rearrange("p (i j) x (dy dx) -> p i j x dy dx", i=SIDE, dy=WIN)
+            everything = to_dy is None and to_dx is None
             for i, src, dst in folds:
-                if i0 <= i < i1:
+                if i0 <= i < i1 and (everything or dst == to_dy):
                     engine.tensor_tensor(
                         out=view[:, i, :, :, dst, :],
                         in0=view[:, i, :, :, dst, :],
@@ -154,12 +180,13 @@ def tile_sam_pb_kernel(tc, logits, x, w3c_words, w3c_scales, b3c, out):
                         op=ALU.add,
                     )
             for j, src, dst in folds:
-                engine.tensor_tensor(
-                    out=view[:, i0:i1, j, :, :, dst],
-                    in0=view[:, i0:i1, j, :, :, dst],
-                    in1=view[:, i0:i1, j, :, :, src],
-                    op=ALU.add,
-                )
+                if everything or dst == to_dx:
+                    engine.tensor_tensor(
+                        out=view[:, i0:i1, j, :, :, dst],
+                        in0=view[:, i0:i1, j, :, :, dst],
+                        in1=view[:, i0:i1, j, :, :, src],
+                        op=ALU.add,
+                    )
 
         def invert(total):
             inv_total = stream.tile([P, HW, 2], F32, name="inv_total")
@@ -217,12 +244,12 @@ def tile_sam_pb_kernel(tc, logits, x, w3c_words, w3c_scales, b3c, out):
             nc.vector.memset(w_scales[:].rearrange("p g n -> p (g n)").bitcast(I32), 0)
 
             x_raw = front.tile([P, B, PASSES, PACK, HW], BF16)
-            nc.scalar.dma_start(
+            load_logits(0, 0)
+            load_logits(0, 1)
+            nc.sync.dma_start(
                 out=x_raw[:], in_=x.rearrange("b (g p t) i j -> p b g t (i j)", g=PASSES, p=P, t=PACK)
             )
             nc.scalar.dma_start(out=bias_bf[:], in_=b3c.rearrange("(g r s) -> r g s", g=HEAD_GROUPS, r=P))
-            load_logits(0, 0)
-            load_logits(0, 1)
             for half in range(2):
                 for r in range(4):
                     nc.sync.dma_start(
@@ -240,32 +267,36 @@ def tile_sam_pb_kernel(tc, logits, x, w3c_words, w3c_scales, b3c, out):
             for xb in range(2):
                 load_logits(3, xb)
 
-            for i0, i1 in halves:
-                maximum(0, i0, i1)
-                numerators(0, e_ready, total_ready, i0, i1)
-
             x_grouped = front.tile([P, PASSES, B * HW, PACK], BF16, align_bytes=64)
-            for g in range(PASSES):
-                for pair in range(PAIRS):
-                    nc.vector.tensor_copy(
-                        out=x_grouped[:, g, P * pair : P * (pair + 1), :].rearrange("p (n x) t -> p n x t", x=2),
+
+            def quantise(pair, engine):
+                cols = slice(P * pair, P * (pair + 1))
+                for g in range(PASSES):
+                    engine.tensor_copy(
+                        out=x_grouped[:, g, cols, :].rearrange("p (n x) t -> p n x t", x=2),
                         in_=x_raw[:, 2 * pair : 2 * pair + 2, g].rearrange("p x t n -> p n x t"),
                     )
-            for g in range(PASSES):
-                nc.vector.quantize_mx(
-                    out=x_codes[:, g, :].bitcast(FP8X4),
-                    scales=x_scales[:, g, :],
-                    in_=x_grouped[:, g].rearrange("p c t -> p (c t)"),
-                )
+                for g in range(PASSES):
+                    nc.vector.quantize_mx(
+                        out=x_codes[:, g, cols].bitcast(FP8X4),
+                        scales=x_scales[:, g, cols],
+                        in_=x_grouped[:, g, cols, :].rearrange("p c t -> p (c t)"),
+                    )
+
+            maximum(0, halves[0][0], halves[0][1])
+            numerators(0, e_ready, total_ready, halves[0][0], halves[0][1])
+            quantise(0, nc.vector)
+            maximum(0, halves[1][0], halves[1][1])
+            numerators(0, e_ready, total_ready, halves[1][0], halves[1][1])
+            maximum_of_pair(1)
+            quantise(1, nc.gpsimd)
             nc.vector.tensor_copy(out=bias[:], in_=bias_bf[:])
-            maximum(1, 0, SIDE)
 
         late = ctx.enter_context(tc.tile_pool(name="late", bufs=2))
         x3T = stream.tile([P, SP, P], F32, name="x3T")
         project(0, x3T, 0)
         project(0, x3T, 1)
         x3_ready = heads_to_partitions(x3T, False)
-        fold(e_ready, halves[0][0], halves[0][1], nc.vector)
         fold(e_ready, halves[1][0], halves[1][1], nc.gpsimd)
 
         def finish(u, backs, inv_total):
@@ -305,7 +336,7 @@ def tile_sam_pb_kernel(tc, logits, x, w3c_words, w3c_scales, b3c, out):
             fold_after = max([0] + [place for place, t in enumerate(tasks) if u > 0 and on_gpsimd(t[0])])
             if more:
                 if u > 0:
-                    maximum(u + 1, 0, SIDE)
+                    maximum_of_pair(u + 1)
                 e_ready = stream.tile([P, HW, 2, PITCH], F32, name="e")
                 total_ready = stream.tile([P, HW, 2], F32, name="total")
                 numerators(u + 1, e_ready, total_ready, 0, SIDE)
@@ -318,6 +349,10 @@ def tile_sam_pb_kernel(tc, logits, x, w3c_words, w3c_scales, b3c, out):
                 j0, j1 = inside(dx)
                 prod = prod_tiles[(dx, uses[dx] % PROD_BUFS)]
                 uses[dx] = uses[dx] + 1
+                if u == 0 and place < KK and dx == 0:
+                    fold(e, halves[0][0], halves[0][1], nc.vector, to_dy=dy)
+                if u == 0 and place < WIN:
+                    fold(e, halves[0][0], halves[0][1], nc.vector, to_dx=dx)
                 if u > 0 and on_gpsimd(l):
                     nc.gpsimd.tensor_tensor(
                         out=prod[:, i0:i1, j0:j1, :, :],

@@ -29,8 +29,9 @@ BANKS = SIDE // BANK_ROWS
 PITCH = 52
 SH = SP // 2
 PROD_BUFS = 2
-GP_EVERY = 6
-FINISH_AFTER = 6
+OVER = (PAD, PAD + 2)
+GP_ROW_OFFSETS = 3
+FOLD_SHARES = {2: 8, 3: 11, 4: 10, 5: 7}
 
 FLOPS = 2 * B * HW * CIN * COUT + 2 * B * COUT * HW * KK
 
@@ -53,25 +54,8 @@ def outside_offsets():
     return found
 
 
-def on_gpsimd(l):
-    return l // WIN <= PAD and l % WIN == PAD
-
-
 def inside(d):
     return max(0, PAD - d), min(SIDE, SIDE + PAD - d)
-
-
-def product_tasks(ranges, with_gpsimd):
-    tasks = []
-    for r0, r1 in ranges:
-        mine = [(l, max(r0, inside(l // WIN)[0]), min(r1, inside(l // WIN)[1])) for l in range(KK)]
-        vector_list = [t for t in mine if not (with_gpsimd and on_gpsimd(t[0]))]
-        gpsimd_list = [t for t in mine if with_gpsimd and on_gpsimd(t[0])]
-        for k, t in enumerate(vector_list):
-            tasks.append(t)
-            if k % GP_EVERY == GP_EVERY - 1 and k // GP_EVERY < len(gpsimd_list):
-                tasks.append(gpsimd_list[k // GP_EVERY])
-    return tasks
 
 
 def tile_sam_pb_kernel(tc, logits, x, w3c_words, w3c_scales, b3c, out):
@@ -94,7 +78,7 @@ def tile_sam_pb_kernel(tc, logits, x, w3c_words, w3c_scales, b3c, out):
 
         prod_tiles = {}
         uses = {}
-        for dx in range(WIN):
+        for dx in range(1, WIN - 1):
             j0, j1 = inside(dx)
             uses[dx] = 0
             for k in range(PROD_BUFS):
@@ -104,6 +88,8 @@ def tile_sam_pb_kernel(tc, logits, x, w3c_words, w3c_scales, b3c, out):
                 if j1 < SIDE:
                     nc.gpsimd.memset(t[:, :, j1:SIDE, :, :], 0.0)
                 prod_tiles[(dx, k)] = t
+        pair_tiles = [keep.tile([P, SIDE, SIDE, 2, SP], F32, name="pair_%d" % k) for k in range(PROD_BUFS)]
+        over_tiles = [keep.tile([P, SIDE, OVER[1] - OVER[0], 2, SP], F32, name="over_%d" % k) for k in range(PROD_BUFS)]
 
         lg = [keep.tile([P, 2, KK, HW], BF16, name="lg%d" % u) for u in range(len(units))]
         minus_top = [keep.tile([P, HW, 2], F32, name="minus_top%d" % u) for u in range(len(units))]
@@ -168,25 +154,24 @@ def tile_sam_pb_kernel(tc, logits, x, w3c_words, w3c_scales, b3c, out):
                         accum_out=total[:, n, xb : xb + 1],
                     )
 
-        def fold(e, i0, i1, engine, to_dy=None, to_dx=None):
+        def fold_steps(e, i0, i1, to_dy=None, to_dx=None):
             view = e[:, :, :, 0:KK].rearrange("p (i j) x (dy dx) -> p i j x dy dx", i=SIDE, dy=WIN)
             everything = to_dy is None and to_dx is None
+            steps = []
             for i, src, dst in folds:
                 if i0 <= i < i1 and (everything or dst == to_dy):
-                    engine.tensor_tensor(
-                        out=view[:, i, :, :, dst, :],
-                        in0=view[:, i, :, :, dst, :],
-                        in1=view[:, i, :, :, src, :],
-                        op=ALU.add,
-                    )
+                    steps.append((view[:, i, :, :, dst, :], view[:, i, :, :, src, :]))
             for j, src, dst in folds:
                 if everything or dst == to_dx:
-                    engine.tensor_tensor(
-                        out=view[:, i0:i1, j, :, :, dst],
-                        in0=view[:, i0:i1, j, :, :, dst],
-                        in1=view[:, i0:i1, j, :, :, src],
-                        op=ALU.add,
-                    )
+                    steps.append((view[:, i0:i1, j, :, :, dst], view[:, i0:i1, j, :, :, src]))
+            return steps
+
+        def add_onto(steps, engine):
+            for target, source in steps:
+                engine.tensor_tensor(out=target, in0=target, in1=source, op=ALU.add)
+
+        def fold(e, i0, i1, engine, to_dy=None, to_dx=None):
+            add_onto(fold_steps(e, i0, i1, to_dy, to_dx), engine)
 
         def invert(total):
             inv_total = stream.tile([P, HW, 2], F32, name="inv_total")
@@ -329,11 +314,12 @@ def tile_sam_pb_kernel(tc, logits, x, w3c_words, w3c_scales, b3c, out):
             e, total = e_ready, total_ready
             x3, x3_sb = x3_ready
             more = u + 1 < len(units)
-            tasks = product_tasks(halves if u == 0 else [(0, SIDE)], u > 0)
-            rows_of = [(place, i) for place, t in enumerate(tasks) for i in range(t[1], t[2])]
-            first = [min([k for k, (place, i) in enumerate(rows_of) if i // BANK_ROWS == bank]) for bank in range(BANKS)]
-            last = [max([k for k, (place, i) in enumerate(rows_of) if i // BANK_ROWS == bank]) for bank in range(BANKS)]
-            fold_after = max([0] + [place for place, t in enumerate(tasks) if u > 0 and on_gpsimd(t[0])])
+            ranges = halves if u == 0 else [(0, SIDE)]
+            blocks = [(dy, max(r0, inside(dy)[0]), min(r1, inside(dy)[1])) for r0, r1 in ranges for dy in range(WIN)]
+            row_order = [i for dy, i0, i1 in blocks for tile_no in range(WIN - 1) for i in range(i0, i1)]
+            first = [min([k for k, i in enumerate(row_order) if i // BANK_ROWS == bank]) for bank in range(BANKS)]
+            last = [max([k for k, i in enumerate(row_order) if i // BANK_ROWS == bank]) for bank in range(BANKS)]
+            next_folds = []
             if more:
                 if u > 0:
                     maximum_of_pair(u + 1)
@@ -341,54 +327,87 @@ def tile_sam_pb_kernel(tc, logits, x, w3c_words, w3c_scales, b3c, out):
                 total_ready = stream.tile([P, HW, 2], F32, name="total")
                 numerators(u + 1, e_ready, total_ready, 0, SIDE)
                 x3T = stream.tile([P, SP, P], F32, name="x3T")
+                for r0, r1 in halves:
+                    next_folds.extend(fold_steps(e_ready, r0, r1))
             by_pos = e[:].rearrange("p (i j) x l -> p i j x l", i=SIDE)
             sums = [sum_psum.tile([P, BANK_ROWS, P], F32, name="sums%d" % bank) for bank in range(BANKS)]
-            k = 0
-            for place, (l, i0, i1) in enumerate(tasks):
-                dy, dx = divmod(l, WIN)
-                j0, j1 = inside(dx)
-                prod = prod_tiles[(dx, uses[dx] % PROD_BUFS)]
-                uses[dx] = uses[dx] + 1
-                if u == 0 and place < KK and dx == 0:
-                    fold(e, halves[0][0], halves[0][1], nc.vector, to_dy=dy)
-                if u == 0 and place < WIN:
-                    fold(e, halves[0][0], halves[0][1], nc.vector, to_dx=dx)
-                if u > 0 and on_gpsimd(l):
-                    nc.gpsimd.tensor_tensor(
-                        out=prod[:, i0:i1, j0:j1, :, :],
-                        in0=x3_sb[:, i0 + dy - PAD : i1 + dy - PAD, j0 + dx - PAD : j1 + dx - PAD, :, :],
-                        in1=by_pos[:, i0:i1, j0:j1, :, l].unsqueeze(4).to_broadcast([P, i1 - i0, j1 - j0, 2, SP]),
-                        op=ALU.mult,
-                    )
-                else:
-                    for h in range(SP // SH):
-                        nc.vector.tensor_tensor(
-                            out=prod[:, i0:i1, j0:j1, :, SH * h : SH * (h + 1)],
-                            in0=x3[h][:, i0 + dy - PAD : i1 + dy - PAD, j0 + dx - PAD : j1 + dx - PAD, :, :],
-                            in1=by_pos[:, i0:i1, j0:j1, :, l].unsqueeze(4).to_broadcast([P, i1 - i0, j1 - j0, 2, SH]),
-                            op=ALU.mult,
-                        )
+            done = [0]
+
+            def add_up(tile, i0, i1):
                 for i in range(i0, i1):
                     bank = i // BANK_ROWS
                     nc.tensor.matmul(
                         out=sums[bank][:, i % BANK_ROWS, :],
-                        lhsT=prod[:, i].rearrange("p j x s -> p (j x s)"),
+                        lhsT=tile[:, i].rearrange("p j x s -> p (j x s)"),
                         rhs=identity[:],
                         is_transpose=True,
-                        start=(k == first[bank]),
-                        stop=(k == last[bank]),
+                        start=(done[0] == first[bank]),
+                        stop=(done[0] == last[bank]),
                     )
-                    k += 1
-                if place == FINISH_AFTER and waiting is not None:
+                    done[0] = done[0] + 1
+
+            def multiply(tile, c0, dy, dx, i0, i1, j0, j1):
+                for h in range(SP // SH):
+                    nc.vector.tensor_tensor(
+                        out=tile[:, i0:i1, c0 : c0 + j1 - j0, :, SH * h : SH * (h + 1)],
+                        in0=x3[h][:, i0 + dy - PAD : i1 + dy - PAD, j0 + dx - PAD : j1 + dx - PAD, :, :],
+                        in1=by_pos[:, i0:i1, j0:j1, :, WIN * dy + dx]
+                        .unsqueeze(4)
+                        .to_broadcast([P, i1 - i0, j1 - j0, 2, SH]),
+                        op=ALU.mult,
+                    )
+
+            for b, (dy, i0, i1) in enumerate(blocks):
+                if u == 0 and b < WIN:
+                    fold(e, halves[0][0], halves[0][1], nc.vector, to_dy=dy)
+                middle = prod_tiles[(PAD, uses[PAD] % PROD_BUFS)]
+                uses[PAD] = uses[PAD] + 1
+                by_gpsimd = u > 0 and dy < GP_ROW_OFFSETS
+                if by_gpsimd:
+                    nc.gpsimd.tensor_tensor(
+                        out=middle[:, i0:i1, :, :, :],
+                        in0=x3_sb[:, i0 + dy - PAD : i1 + dy - PAD, :, :, :],
+                        in1=by_pos[:, i0:i1, :, :, WIN * dy + PAD].unsqueeze(4).to_broadcast([P, i1 - i0, SIDE, 2, SP]),
+                        op=ALU.mult,
+                    )
+                both = pair_tiles[b % PROD_BUFS]
+                over = over_tiles[b % PROD_BUFS]
+                if u == 0 and b == 0:
+                    fold(e, halves[0][0], halves[0][1], nc.vector, to_dx=0)
+                    fold(e, halves[0][0], halves[0][1], nc.vector, to_dx=WIN - 1)
+                multiply(both, OVER[0], dy, 0, i0, i1, OVER[0], SIDE)
+                multiply(both, 0, dy, WIN - 1, i0, i1, 0, OVER[0])
+                multiply(over, 0, dy, WIN - 1, i0, i1, OVER[0], OVER[1])
+                for dx in (1, 2, 4, 5, PAD):
+                    j0, j1 = inside(dx)
+                    if u == 0 and b == 0:
+                        fold(e, halves[0][0], halves[0][1], nc.vector, to_dx=dx)
+                    if dx == PAD:
+                        prod = middle
+                    else:
+                        prod = prod_tiles[(dx, uses[dx] % PROD_BUFS)]
+                        uses[dx] = uses[dx] + 1
+                    if dx != PAD or not by_gpsimd:
+                        multiply(prod, j0, dy, dx, i0, i1, j0, j1)
+                    if dx == 1:
+                        add_onto(
+                            [(both[:, i0:i1, OVER[0] : OVER[1], :, :], over[:, i0:i1, :, :, :])],
+                            nc.vector if u == 0 else nc.gpsimd,
+                        )
+                    add_up(prod, i0, i1)
+                add_up(both, i0, i1)
+                if b == 0 and waiting is not None:
                     finish(waiting[0], waiting[1], waiting[2])
-                if more and place == fold_after:
-                    for r0, r1 in halves:
-                        fold(e_ready, r0, r1, nc.gpsimd)
-                if more and place == (3 * len(tasks)) // 10:
+                if u == 0 and b == 0:
+                    add_onto(next_folds, nc.gpsimd)
+                if u > 0 and more and dy in FOLD_SHARES:
+                    add_onto(next_folds[0 : FOLD_SHARES[dy]], nc.gpsimd)
+                    next_folds = next_folds[FOLD_SHARES[dy] :]
+                if more and b == (3 * len(blocks)) // 10:
                     project(u + 1, x3T, 0)
-                if more and place == (6 * len(tasks)) // 10:
+                if more and b == (6 * len(blocks)) // 10:
                     project(u + 1, x3T, 1)
-                if more and place == (8 * len(tasks)) // 10:
+                if more and b == (8 * len(blocks)) // 10:
                     x3_ready = heads_to_partitions(x3T, True)
             inv_total = invert(total)
 

@@ -64,6 +64,7 @@ def tile_sam_pb_kernel(tc, logits, x, w3c_words, w3c_scales, b3c, out):
     units = [(hg, pair) for hg in range(HEAD_GROUPS) for pair in range(PAIRS)]
     halves = [(0, SIDE // 2), (SIDE // 2, SIDE)]
     with ExitStack() as ctx:
+        ctx.enter_context(tc.manual_schedule())
         keep = ctx.enter_context(tc.tile_pool(name="keep", bufs=1))
         stream = ctx.enter_context(tc.tile_pool(name="stream", bufs=2))
         front_psum = ctx.enter_context(tc.psum_pool(name="front_psum", bufs=2))
@@ -98,49 +99,48 @@ def tile_sam_pb_kernel(tc, logits, x, w3c_words, w3c_scales, b3c, out):
             hg, pair = units[u]
             nc.sync.dma_start(out=lg[u][:, xb], in_=logits[2 * pair + xb, P * hg : P * (hg + 1)])
 
-        def maximum(u, i0, i1):
-            n0, n1 = SIDE * i0, SIDE * i1
-            for xb in range(2):
-                top = stream.tile([P, KK // 2, n1 - n0], BF16, name="top")
-                nc.vector.tensor_tensor(
-                    out=top[:],
-                    in0=lg[u][:, xb, 0 : KK // 2, n0:n1],
-                    in1=lg[u][:, xb, KK // 2 + 1 : KK, n0:n1],
-                    op=ALU.max,
-                )
-                rows = KK // 2
-                while rows > 1:
-                    half = rows // 2
-                    nc.vector.tensor_tensor(
-                        out=top[:, 0:half, :], in0=top[:, 0:half, :], in1=top[:, rows - half : rows, :], op=ALU.max
-                    )
-                    rows = rows - half
-                nc.vector.tensor_tensor(
-                    out=top[:, 0:1, :], in0=top[:, 0:1, :], in1=lg[u][:, xb, KK // 2 : KK // 2 + 1, n0:n1], op=ALU.max
-                )
-                nc.vector.tensor_scalar_mul(out=minus_top[u][:, n0:n1, xb], in0=top[:, 0, :], scalar1=-1.0)
-
-        def maximum_of_pair(u):
-            top = stream.tile([P, 2, KK // 2, HW], BF16, name="top_pair", bufs=1)
-            nc.vector.tensor_tensor(
-                out=top[:], in0=lg[u][:, :, 0 : KK // 2, :], in1=lg[u][:, :, KK // 2 + 1 : KK, :], op=ALU.max
-            )
+        def tree(top, source):
+            steps = [(top, source[:, :, 0 : KK // 2, :], source[:, :, KK // 2 + 1 : KK, :])]
             rows = KK // 2
             while rows > 1:
                 half = rows // 2
-                nc.vector.tensor_tensor(
-                    out=top[:, :, 0:half, :],
-                    in0=top[:, :, 0:half, :],
-                    in1=top[:, :, rows - half : rows, :],
-                    op=ALU.max,
-                )
+                steps.append((top[:, :, 0:half, :], top[:, :, 0:half, :], top[:, :, rows - half : rows, :]))
                 rows = rows - half
-            nc.vector.tensor_tensor(
-                out=top[:, :, 0:1, :], in0=top[:, :, 0:1, :], in1=lg[u][:, :, KK // 2 : KK // 2 + 1, :], op=ALU.max
-            )
-            nc.vector.tensor_scalar_mul(
-                out=minus_top[u][:].rearrange("p n x -> p x n"), in0=top[:, :, 0, :], scalar1=-1.0
-            )
+            steps.append((top[:, :, 0:1, :], top[:, :, 0:1, :], source[:, :, KK // 2 : KK // 2 + 1, :]))
+            return steps
+
+        def larger(step):
+            nc.vector.tensor_tensor(out=step[0], in0=step[1], in1=step[2], op=ALU.max)
+
+        def maximum(u, i0, i1):
+            n0, n1 = SIDE * i0, SIDE * i1
+            tops = [stream.tile([P, 1, KK // 2, n1 - n0], BF16, name="top") for xb in range(2)]
+            trees = [tree(tops[xb][:], lg[u][:, xb : xb + 1, :, n0:n1]) for xb in range(2)]
+            for pair_of_steps in zip(trees[0], trees[1]):
+                for step in pair_of_steps:
+                    larger(step)
+            for xb in range(2):
+                nc.vector.tensor_scalar_mul(out=minus_top[u][:, n0:n1, xb], in0=tops[xb][:, 0, 0, :], scalar1=-1.0)
+
+        def maximum_of_pair_steps(u):
+            top = stream.tile([P, 2, KK // 2, HW], BF16, name="top_pair", bufs=1)
+            return [(step, None) for step in tree(top[:], lg[u][:])] + [(None, (u, top))]
+
+        def one_step(calls):
+            if len(calls) > 0:
+                step, last = calls[0]
+                if last is None:
+                    larger(step)
+                else:
+                    nc.vector.tensor_scalar_mul(
+                        out=minus_top[last[0]][:].rearrange("p n x -> p x n"), in0=last[1][:, :, 0, :], scalar1=-1.0
+                    )
+                calls.remove(calls[0])
+
+        def maximum_of_pair(u):
+            calls = maximum_of_pair_steps(u)
+            while len(calls) > 0:
+                one_step(calls)
 
         def numerators(u, e, total, i0, i1):
             for n in range(SIDE * i0, SIDE * i1):
@@ -321,8 +321,6 @@ def tile_sam_pb_kernel(tc, logits, x, w3c_words, w3c_scales, b3c, out):
             last = [max([k for k, i in enumerate(row_order) if i // BANK_ROWS == bank]) for bank in range(BANKS)]
             next_folds = []
             if more:
-                if u > 0:
-                    maximum_of_pair(u + 1)
                 e_ready = stream.tile([P, HW, 2, PITCH], F32, name="e")
                 total_ready = stream.tile([P, HW, 2], F32, name="total")
                 numerators(u + 1, e_ready, total_ready, 0, SIDE)
@@ -332,6 +330,7 @@ def tile_sam_pb_kernel(tc, logits, x, w3c_words, w3c_scales, b3c, out):
             by_pos = e[:].rearrange("p (i j) x l -> p i j x l", i=SIDE)
             sums = [sum_psum.tile([P, BANK_ROWS, P], F32, name="sums%d" % bank) for bank in range(BANKS)]
             done = [0]
+            maxima_calls = []
 
             def add_up(tile, i0, i1):
                 for i in range(i0, i1):
@@ -389,6 +388,7 @@ def tile_sam_pb_kernel(tc, logits, x, w3c_words, w3c_scales, b3c, out):
                         uses[dx] = uses[dx] + 1
                     if dx != PAD or not by_gpsimd:
                         multiply(prod, j0, dy, dx, i0, i1, j0, j1)
+                    one_step(maxima_calls)
                     if dx == 1:
                         add_onto(
                             [(both[:, i0:i1, OVER[0] : OVER[1], :, :], over[:, i0:i1, :, :, :])],
@@ -403,6 +403,8 @@ def tile_sam_pb_kernel(tc, logits, x, w3c_words, w3c_scales, b3c, out):
                 if u > 0 and more and dy in FOLD_SHARES:
                     add_onto(next_folds[0 : FOLD_SHARES[dy]], nc.gpsimd)
                     next_folds = next_folds[FOLD_SHARES[dy] :]
+                if u + 2 < len(units) and b == len(blocks) // 2:
+                    maxima_calls.extend(maximum_of_pair_steps(u + 2))
                 if more and b == (3 * len(blocks)) // 10:
                     project(u + 1, x3T, 0)
                 if more and b == (6 * len(blocks)) // 10:

@@ -30,7 +30,8 @@ PITCH = 52
 SH = SP // 2
 PROD_BUFS = 2
 OVER = (PAD, PAD + 2)
-GP_ROW_OFFSETS = 3
+INNER = (1, 2, 4, 5, PAD)
+GP_ROW_OFFSETS = 4
 FOLD_SHARES = {2: 8, 3: 11, 4: 10, 5: 7}
 
 FLOPS = 2 * B * HW * CIN * COUT + 2 * B * COUT * HW * KK
@@ -357,8 +358,6 @@ def tile_sam_pb_kernel(tc, logits, x, w3c_words, w3c_scales, b3c, out):
                     )
 
             for b, (dy, i0, i1) in enumerate(blocks):
-                if u == 0 and b < WIN:
-                    fold(e, halves[0][0], halves[0][1], nc.vector, to_dy=dy)
                 middle = prod_tiles[(PAD, uses[PAD] % PROD_BUFS)]
                 uses[PAD] = uses[PAD] + 1
                 by_gpsimd = u > 0 and dy < GP_ROW_OFFSETS
@@ -372,15 +371,20 @@ def tile_sam_pb_kernel(tc, logits, x, w3c_words, w3c_scales, b3c, out):
                 both = pair_tiles[b % PROD_BUFS]
                 over = over_tiles[b % PROD_BUFS]
                 if u == 0 and b == 0:
+                    fold(e, halves[0][0], halves[0][1], nc.vector, to_dy=0)
+                    fold(e, halves[0][0], halves[0][1], nc.vector, to_dy=1)
                     fold(e, halves[0][0], halves[0][1], nc.vector, to_dx=0)
                     fold(e, halves[0][0], halves[0][1], nc.vector, to_dx=WIN - 1)
+                    fold(e, halves[0][0], halves[0][1], nc.vector, to_dx=INNER[0])
                 multiply(both, OVER[0], dy, 0, i0, i1, OVER[0], SIDE)
                 multiply(both, 0, dy, WIN - 1, i0, i1, 0, OVER[0])
                 multiply(over, 0, dy, WIN - 1, i0, i1, OVER[0], OVER[1])
-                for dx in (1, 2, 4, 5, PAD):
+                for turn, dx in enumerate(INNER):
                     j0, j1 = inside(dx)
-                    if u == 0 and b == 0:
-                        fold(e, halves[0][0], halves[0][1], nc.vector, to_dx=dx)
+                    if u == 0 and b == 0 and turn + 1 < len(INNER):
+                        fold(e, halves[0][0], halves[0][1], nc.vector, to_dx=INNER[turn + 1])
+                    if u == 0 and 0 < b < WIN - 1 and turn == 2:
+                        fold(e, halves[0][0], halves[0][1], nc.vector, to_dy=dy + 1)
                     if dx == PAD:
                         prod = middle
                     else:

@@ -32,7 +32,7 @@ PROD_BUFS = 2
 OVER = (PAD, PAD + 2)
 INNER = (1, 2, 4, 5, PAD)
 GP_ROW_OFFSETS = 4
-FOLD_SHARES = {2: 8, 3: 11, 4: 10, 5: 7}
+FOLD_SHARES = {2: 6, 3: 8, 4: 6, 5: 4}
 
 FLOPS = 2 * B * HW * CIN * COUT + 2 * B * COUT * HW * KK
 
@@ -326,8 +326,15 @@ def tile_sam_pb_kernel(tc, logits, x, w3c_words, w3c_scales, b3c, out):
                 total_ready = stream.tile([P, HW, 2], F32, name="total")
                 numerators(u + 1, e_ready, total_ready, 0, SIDE)
                 x3T = stream.tile([P, SP, P], F32, name="x3T")
-                for r0, r1 in halves:
-                    next_folds.extend(fold_steps(e_ready, r0, r1))
+                if u == 0:
+                    for r0, r1 in halves:
+                        next_folds.extend(fold_steps(e_ready, r0, r1))
+                else:
+                    for i in range(SIDE):
+                        for to_dy in range(WIN):
+                            next_folds.extend(fold_steps(e_ready, i, i + 1, to_dy=to_dy))
+                    for to_dx in range(WIN):
+                        next_folds.extend(fold_steps(e_ready, 0, SIDE, to_dx=to_dx))
             by_pos = e[:].rearrange("p (i j) x l -> p i j x l", i=SIDE)
             sums = [sum_psum.tile([P, BANK_ROWS, P], F32, name="sums%d" % bank) for bank in range(BANKS)]
             done = [0]

from contextlib import ExitStack

import concourse.mybir as mybir
from concourse.masks import make_identity

F32 = mybir.dt.float32
BF16 = mybir.dt.bfloat16
I32 = mybir.dt.int32
U32 = mybir.dt.uint32
U8 = mybir.dt.uint8
FP8X4 = mybir.dt.float8_e4m3fn_x4
FP4X4 = mybir.dt.float4_e2m1fn_x4
ALU = mybir.AluOpType
ACT = mybir.ActivationFunctionType

P = 128
PACK = 4
K_PASS = P * PACK
B, CIN, SIDE, COUT, SP, WIN = 4, 2048, 8, 2048, 8, 7
HW = SIDE * SIDE
KK = WIN * WIN
PAD = WIN // 2
PASSES = CIN // K_PASS
N_TILE = 512
HEAD_GROUPS = COUT // SP // P
PAIRS = B // 2
BANK_ROWS = N_TILE // P
BANKS = SIDE // BANK_ROWS
PITCH = 52
SH = SP // 2
PROD_BUFS = 2
OVER = (PAD, PAD + 2)
INNER = (1, 2, 4, 5, PAD)
GP_ROW_OFFSETS = 4
FOLD_SHARES = {2: 6, 3: 8, 4: 6, 5: 4}

FLOPS = 2 * B * HW * CIN * COUT + 2 * B * COUT * HW * KK


def mirror(u):
    if u < 0:
        return -u
    if u > SIDE - 1:
        return 2 * (SIDE - 1) - u
    return u


def outside_offsets():
    found = []
    for i in range(SIDE):
        for dy in range(WIN):
            u = i + dy - PAD
            if mirror(u) != u:
                found.append((i, dy, mirror(u) - i + PAD))
    return found


def inside(d):
    return max(0, PAD - d), min(SIDE, SIDE + PAD - d)


def tile_sam_pb_kernel(tc, logits, x, w3c_words, w3c_scales, b3c, out):
    nc = tc.nc
    folds = outside_offsets()
    units = [(hg, pair) for hg in range(HEAD_GROUPS) for pair in range(PAIRS)]
    halves = [(0, SIDE // 2), (SIDE // 2, SIDE)]
    with ExitStack() as ctx:
        ctx.enter_context(tc.manual_schedule())
        keep = ctx.enter_context(tc.tile_pool(name="keep", bufs=1))
        stream = ctx.enter_context(tc.tile_pool(name="stream", bufs=2))
        front_psum = ctx.enter_context(tc.psum_pool(name="front_psum", bufs=2))
        x3_psum = ctx.enter_context(tc.psum_pool(name="x3_psum", bufs=2))
        sum_psum = ctx.enter_context(tc.psum_pool(name="sum_psum", bufs=1))

        identity = keep.tile([P, P], F32)
        make_identity(nc, identity[:])
        warm = keep.tile([P, 1], F32)
        nc.vector.memset(warm[:], 0.0)
        nc.scalar.activation(out=warm[:], in_=warm[:], func=ACT.Exp)

        prod_tiles = {}
        uses = {}
        for dx in range(1, WIN - 1):
            j0, j1 = inside(dx)
            uses[dx] = 0
            for k in range(PROD_BUFS):
                t = keep.tile([P, SIDE, SIDE, 2, SP], F32, name="prod_%d_%d" % (dx, k))
                if j0 > 0:
                    nc.gpsimd.memset(t[:, :, 0:j0, :, :], 0.0)
                if j1 < SIDE:
                    nc.gpsimd.memset(t[:, :, j1:SIDE, :, :], 0.0)
                prod_tiles[(dx, k)] = t
        pair_tiles = [keep.tile([P, SIDE, SIDE, 2, SP], F32, name="pair_%d" % k) for k in range(PROD_BUFS)]
        over_tiles = [keep.tile([P, SIDE, OVER[1] - OVER[0], 2, SP], F32, name="over_%d" % k) for k in range(PROD_BUFS)]

        lg = [keep.tile([P, 2, KK, HW], BF16, name="lg%d" % u) for u in range(len(units))]
        minus_top = [keep.tile([P, HW, 2], F32, name="minus_top%d" % u) for u in range(len(units))]

        def load_logits(u, xb):
            hg, pair = units[u]
            nc.sync.dma_start(out=lg[u][:, xb], in_=logits[2 * pair + xb, P * hg : P * (hg + 1)])

        def tree(top, source):
            steps = [(top, source[:, :, 0 : KK // 2, :], source[:, :, KK // 2 + 1 : KK, :])]
            rows = KK // 2
            while rows > 1:
                half = rows // 2
                steps.append((top[:, :, 0:half, :], top[:, :, 0:half, :], top[:, :, rows - half : rows, :]))
                rows = rows - half
            steps.append((top[:, :, 0:1, :], top[:, :, 0:1, :], source[:, :, KK // 2 : KK // 2 + 1, :]))
            return steps

        def larger(step):
            nc.vector.tensor_tensor(out=step[0], in0=step[1], in1=step[2], op=ALU.max)

        def maximum(u, i0, i1):
            n0, n1 = SIDE * i0, SIDE * i1
            tops = [stream.tile([P, 1, KK // 2, n1 - n0], BF16, name="top") for xb in range(2)]
            trees = [tree(tops[xb][:], lg[u][:, xb : xb + 1, :, n0:n1]) for xb in range(2)]
            for pair_of_steps in zip(trees[0], trees[1]):
                for step in pair_of_steps:
                    larger(step)
            for xb in range(2):
                nc.vector.tensor_scalar_mul(out=minus_top[u][:, n0:n1, xb], in0=tops[xb][:, 0, 0, :], scalar1=-1.0)

        def maximum_of_pair_steps(u):
            top = stream.tile([P, 2, KK // 2, HW], BF16, name="top_pair", bufs=1)
            return [(step, None) for step in tree(top[:], lg[u][:])] + [(None, (u, top))]

        def one_step(calls):
            if len(calls) > 0:
                step, last = calls[0]
                if last is None:
                    larger(step)
                else:
                    nc.vector.tensor_scalar_mul(
                        out=minus_top[last[0]][:].rearrange("p n x -> p x n"), in0=last[1][:, :, 0, :], scalar1=-1.0
                    )
                calls.remove(calls[0])

        def maximum_of_pair(u):
            calls = maximum_of_pair_steps(u)
            while len(calls) > 0:
                one_step(calls)

        def numerators(u, e, total, i0, i1):
            for n in range(SIDE * i0, SIDE * i1):
                for xb in range(2):
                    nc.scalar.activation(
                        out=e[:, n, xb, 0:KK],
                        in_=lg[u][:, xb, :, n],
                        func=ACT.Exp,
                        bias=minus_top[u][:, n, xb : xb + 1],
                        scale=1.0,
                        accum_out=total[:, n, xb : xb + 1],
                    )

        def fold_steps(e, i0, i1, to_dy=None, to_dx=None):
            view = e[:, :, :, 0:KK].rearrange("p (i j) x (dy dx) -> p i j x dy dx", i=SIDE, dy=WIN)
            everything = to_dy is None and to_dx is None
            steps = []
            for i, src, dst in folds:
                if i0 <= i < i1 and (everything or dst == to_dy):
                    steps.append((view[:, i, :, :, dst, :], view[:, i, :, :, src, :]))
            for j, src, dst in folds:
                if everything or dst == to_dx:
                    steps.append((view[:, i0:i1, j, :, :, dst], view[:, i0:i1, j, :, :, src]))
            return steps

        def add_onto(steps, engine):
            for target, source in steps:
                engine.tensor_tensor(out=target, in0=target, in1=source, op=ALU.add)

        def fold(e, i0, i1, engine, to_dy=None, to_dx=None):
            add_onto(fold_steps(e, i0, i1, to_dy, to_dx), engine)

        def invert(total):
            inv_total = stream.tile([P, HW, 2], F32, name="inv_total")
            nc.vector.reciprocal(out=inv_total[:], in_=total[:])
            return inv_total

        x_codes = keep.tile([P, PASSES, B * HW], U32, align_bytes=64)
        x_scales = keep.tile([P, PASSES, B * HW], U8, align_bytes=64)
        w_scales = keep.tile([P, PASSES, COUT], U8, align_bytes=64)
        w_words = keep.tile([P, PASSES, 2 * COUT], U8, align_bytes=64)
        heads_per_tile = N_TILE // SP

        def project(u, x3T, part):
            hg, pair = units[u]
            cols = slice(P * pair, P * (pair + 1))
            ot = 2 * hg + part
            acc = front_psum.tile([P, N_TILE], F32, name="front")
            for g in range(PASSES):
                nc.tensor.matmul_mx(
                    out=acc[:],
                    lhsT=x_codes[:, g, cols].bitcast(FP8X4),
                    lhsT_scale=x_scales[:, g, cols],
                    rhs=w_words[:, g, 2 * N_TILE * ot : 2 * N_TILE * (ot + 1)].bitcast(FP4X4),
                    rhs_scale=w_scales[:, g, N_TILE * ot : N_TILE * (ot + 1)],
                    start=(g == 0),
                    stop=(g == PASSES - 1),
                )
            target = x3T[:, :, heads_per_tile * part : heads_per_tile * (part + 1)]
            if u == 0:
                nc.vector.tensor_copy(out=target, in_=acc[:].rearrange("p (h s) -> p s h", s=SP))
            else:
                nc.scalar.copy(out=target, in_=acc[:].rearrange("p (h s) -> p s h", s=SP))

        def heads_to_partitions(x3T, for_gpsimd):
            banks = [x3_psum.tile([P, SIDE, SIDE, 2, SH], F32, name="x3_%d" % h) for h in range(SP // SH)]
            for s in range(SP):
                nc.tensor.transpose(
                    banks[s // SH][:].rearrange("p i j x s -> p (i j x) s")[:, :, s % SH],
                    x3T[:, s, :],
                    identity[:],
                )
            x3_sb = None
            if for_gpsimd:
                x3_sb = late.tile([P, SIDE, SIDE, 2, SP], F32, name="x3_sb")
                for h in range(SP // SH):
                    nc.scalar.copy(out=x3_sb[:, :, :, :, SH * h : SH * (h + 1)], in_=banks[h][:])
            return banks, x3_sb

        bias_bf = keep.tile([P, HEAD_GROUPS, SP], BF16)
        bias = keep.tile([P, HEAD_GROUPS, SP], F32)
        e_ready = stream.tile([P, HW, 2, PITCH], F32, name="e")
        total_ready = stream.tile([P, HW, 2], F32, name="total")

        with tc.tile_pool(name="front", bufs=1) as front:
            nc.vector.memset(w_scales[:].rearrange("p g n -> p (g n)").bitcast(I32), 0)

            x_raw = front.tile([P, B, PASSES, PACK, HW], BF16)
            load_logits(0, 0)
            load_logits(0, 1)
            nc.sync.dma_start(
                out=x_raw[:], in_=x.rearrange("b (g p t) i j -> p b g t (i j)", g=PASSES, p=P, t=PACK)
            )
            nc.scalar.dma_start(out=bias_bf[:], in_=b3c.rearrange("(g r s) -> r g s", g=HEAD_GROUPS, r=P))
            for half in range(2):
                for r in range(4):
                    nc.sync.dma_start(
                        out=w_scales[32 * half + r : P : 64, :, :].bitcast(I32),
                        in_=w3c_scales[:, 4 * half + r : 16 : 8, :].rearrange("g q n -> q g n").bitcast(I32),
                    )
            for hg in range(HEAD_GROUPS):
                for g in range(PASSES):
                    nc.sync.dma_start(
                        out=w_words[:, g, COUT * hg : COUT * (hg + 1)].bitcast(I32),
                        in_=w3c_words[g][:, COUT * hg : COUT * (hg + 1)].bitcast(I32),
                    )
                for xb in range(2):
                    load_logits(1 + hg, xb)
            for xb in range(2):
                load_logits(3, xb)

            x_grouped = front.tile([P, PASSES, B * HW, PACK], BF16, align_bytes=64)

            def quantise(pair, engine):
                cols = slice(P * pair, P * (pair + 1))
                for g in range(PASSES):
                    engine.tensor_copy(
                        out=x_grouped[:, g, cols, :].rearrange("p (n x) t -> p n x t", x=2),
                        in_=x_raw[:, 2 * pair : 2 * pair + 2, g].rearrange("p x t n -> p n x t"),
                    )
                for g in range(PASSES):
                    nc.vector.quantize_mx(
                        out=x_codes[:, g, cols].bitcast(FP8X4),
                        scales=x_scales[:, g, cols],
                        in_=x_grouped[:, g, cols, :].rearrange("p c t -> p (c t)"),
                    )

            maximum(0, halves[0][0], halves[0][1])
            numerators(0, e_ready, total_ready, halves[0][0], halves[0][1])
            quantise(0, nc.vector)
            maximum(0, halves[1][0], halves[1][1])
            numerators(0, e_ready, total_ready, halves[1][0], halves[1][1])
            maximum_of_pair(1)
            quantise(1, nc.gpsimd)
            nc.vector.tensor_copy(out=bias[:], in_=bias_bf[:])

        late = ctx.enter_context(tc.tile_pool(name="late", bufs=2))
        x3T = stream.tile([P, SP, P], F32, name="x3T")
        project(0, x3T, 0)
        project(0, x3T, 1)
        x3_ready = heads_to_partitions(x3T, False)
        fold(e_ready, halves[1][0], halves[1][1], nc.gpsimd)

        def finish(u, backs, inv_total):
            hg, pair = units[u]
            y = late.tile([P, 2, SP, HW], F32, name="y")
            for bank in range(BANKS):
                positions = slice(SIDE * BANK_ROWS * bank, SIDE * BANK_ROWS * (bank + 1))
                for xb in range(2):
                    nc.vector.tensor_tensor(
                        out=y[:, xb, :, positions].rearrange("p s (i j) -> p s i j", j=SIDE),
                        in0=backs[bank][:, :, :, xb, :].rearrange("p i j s -> p s i j"),
                        in1=inv_total[:, positions, xb]
                        .rearrange("p (i j) -> p i j", j=SIDE)
                        .unsqueeze(1)
                        .to_broadcast([P, SP, BANK_ROWS, SIDE]),
                        op=ALU.mult,
                    )
            for s in range(SP):
                nc.scalar.activation(
                    out=y[:, :, s, :], in_=y[:, :, s, :], func=ACT.Identity, bias=bias[:, hg, s : s + 1], scale=1.0
                )
            for xb in range(2):
                nc.sync.dma_start(
                    out=out[2 * pair + xb, SP * P * hg : SP * P * (hg + 1)].rearrange("(r s) i j -> r (s i j)", s=SP),
                    in_=y[:, xb].rearrange("p s n -> p (s n)"),
                )

        waiting = None
        for u, (hg, pair) in enumerate(units):
            e, total = e_ready, total_ready
            x3, x3_sb = x3_ready
            more = u + 1 < len(units)
            ranges = halves if u == 0 else [(0, SIDE)]
            blocks = [(dy, max(r0, inside(dy)[0]), min(r1, inside(dy)[1])) for r0, r1 in ranges for dy in range(WIN)]
            row_order = [i for dy, i0, i1 in blocks for tile_no in range(WIN - 1) for i in range(i0, i1)]
            first = [min([k for k, i in enumerate(row_order) if i // BANK_ROWS == bank]) for bank in range(BANKS)]
            last = [max([k for k, i in enumerate(row_order) if i // BANK_ROWS == bank]) for bank in range(BANKS)]
            next_folds = []
            if more:
                e_ready = stream.tile([P, HW, 2, PITCH], F32, name="e")
                total_ready = stream.tile([P, HW, 2], F32, name="total")
                numerators(u + 1, e_ready, total_ready, 0, SIDE)
                x3T = stream.tile([P, SP, P], F32, name="x3T")
                if u == 0:
                    for r0, r1 in halves:
                        next_folds.extend(fold_steps(e_ready, r0, r1))
                else:
                    for i in range(SIDE):
                        for to_dy in range(WIN):
                            next_folds.extend(fold_steps(e_ready, i, i + 1, to_dy=to_dy))
                    for to_dx in range(WIN):
                        next_folds.extend(fold_steps(e_ready, 0, SIDE, to_dx=to_dx))
            by_pos = e[:].rearrange("p (i j) x l -> p i j x l", i=SIDE)
            sums = [sum_psum.tile([P, BANK_ROWS, P], F32, name="sums%d" % bank) for bank in range(BANKS)]
            done = [0]
            maxima_calls = []

            def add_up(tile, i0, i1):
                for i in range(i0, i1):
                    bank = i // BANK_ROWS
                    nc.tensor.matmul(
                        out=sums[bank][:, i % BANK_ROWS, :],
                        lhsT=tile[:, i].rearrange("p j x s -> p (j x s)"),
                        rhs=identity[:],
                        is_transpose=True,
                        start=(done[0] == first[bank]),
                        stop=(done[0] == last[bank]),
                    )
                    done[0] = done[0] + 1

            def multiply(tile, c0, dy, dx, i0, i1, j0, j1):
                for h in range(SP // SH):
                    nc.vector.tensor_tensor(
                        out=tile[:, i0:i1, c0 : c0 + j1 - j0, :, SH * h : SH * (h + 1)],
                        in0=x3[h][:, i0 + dy - PAD : i1 + dy - PAD, j0 + dx - PAD : j1 + dx - PAD, :, :],
                        in1=by_pos[:, i0:i1, j0:j1, :, WIN * dy + dx]
                        .unsqueeze(4)
                        .to_broadcast([P, i1 - i0, j1 - j0, 2, SH]),
                        op=ALU.mult,
                    )

            for b, (dy, i0, i1) in enumerate(blocks):
                middle = prod_tiles[(PAD, uses[PAD] % PROD_BUFS)]
                uses[PAD] = uses[PAD] + 1
                by_gpsimd = u > 0 and dy < GP_ROW_OFFSETS
                if by_gpsimd:
                    nc.gpsimd.tensor_tensor(
                        out=middle[:, i0:i1, :, :, :],
                        in0=x3_sb[:, i0 + dy - PAD : i1 + dy - PAD, :, :, :],
                        in1=by_pos[:, i0:i1, :, :, WIN * dy + PAD].unsqueeze(4).to_broadcast([P, i1 - i0, SIDE, 2, SP]),
                        op=ALU.mult,
                    )
                both = pair_tiles[b % PROD_BUFS]
                over = over_tiles[b % PROD_BUFS]
                if u == 0 and b == 0:
                    fold(e, halves[0][0], halves[0][1], nc.vector, to_dy=0)
                    fold(e, halves[0][0], halves[0][1], nc.vector, to_dy=1)
                    fold(e, halves[0][0], halves[0][1], nc.vector, to_dx=0)
                    fold(e, halves[0][0], halves[0][1], nc.vector, to_dx=WIN - 1)
                    fold(e, halves[0][0], halves[0][1], nc.vector, to_dx=INNER[0])
                multiply(both, OVER[0], dy, 0, i0, i1, OVER[0], SIDE)
                multiply(both, 0, dy, WIN - 1, i0, i1, 0, OVER[0])
                multiply(over, 0, dy, WIN - 1, i0, i1, OVER[0], OVER[1])
                for turn, dx in enumerate(INNER):
                    j0, j1 = inside(dx)
                    if u == 0 and b == 0 and turn + 1 < len(INNER):
                        fold(e, halves[0][0], halves[0][1], nc.vector, to_dx=INNER[turn + 1])
                    if u == 0 and 0 < b < WIN - 1 and turn == 2:
                        fold(e, halves[0][0], halves[0][1], nc.vector, to_dy=dy + 1)
                    if dx == PAD:
                        prod = middle
                    else:
                        prod = prod_tiles[(dx, uses[dx] % PROD_BUFS)]
                        uses[dx] = uses[dx] + 1
                    if dx != PAD or not by_gpsimd:
                        multiply(prod, j0, dy, dx, i0, i1, j0, j1)
                    one_step(maxima_calls)
                    if dx == 1:
                        add_onto(
                            [(both[:, i0:i1, OVER[0] : OVER[1], :, :], over[:, i0:i1, :, :, :])],
                            nc.vector if u == 0 else nc.gpsimd,
                        )
                    add_up(prod, i0, i1)
                add_up(both, i0, i1)
                if b == 0 and waiting is not None:
                    finish(waiting[0], waiting[1], waiting[2])
                if u == 0 and b == 0:
                    add_onto(next_folds, nc.gpsimd)
                if u > 0 and more and dy in FOLD_SHARES:
                    add_onto(next_folds[0 : FOLD_SHARES[dy]], nc.gpsimd)
                    next_folds = next_folds[FOLD_SHARES[dy] :]
                if u + 2 < len(units) and b == len(blocks) // 2:
                    maxima_calls.extend(maximum_of_pair_steps(u + 2))
                if more and b == (3 * len(blocks)) // 10:
                    project(u + 1, x3T, 0)
                if more and b == (6 * len(blocks)) // 10:
                    project(u + 1, x3T, 1)
                if more and b == (8 * len(blocks)) // 10:
                    x3_ready = heads_to_partitions(x3T, True)
            inv_total = invert(total)

            backs = []
            for bank in range(BANKS):
                sums_sb = late.tile([P, BANK_ROWS, P], F32, name="sums_sb")
                nc.scalar.copy(out=sums_sb[:], in_=sums[bank][:])
                back = front_psum.tile([P, BANK_ROWS, SIDE, 2, SP], F32, name="front")
                for r in range(BANK_ROWS):
                    nc.tensor.transpose(back[:, r].rearrange("p j x s -> p (j x s)"), sums_sb[:, r, :], identity[:])
                backs.append(back)
            waiting = (u, backs, inv_total)
        finish(waiting[0], waiting[1], waiting[2])
